import numpy as np
import ml_dtypes


def mxq(x, axis, fmt="e4m3"):
    dtype, down = {"e4m3": (ml_dtypes.float8_e4m3fn, 7), "e5m2": (ml_dtypes.float8_e5m2, 14)}[fmt]
    v = np.moveaxis(np.asarray(x, np.float32).astype(ml_dtypes.bfloat16).astype(np.float64), axis, -1)
    blocks = v.reshape(v.shape[:-1] + (-1, 32))
    amax = np.abs(blocks).max(-1, keepdims=True)
    byte = np.maximum(np.where(amax > 0, np.frexp(amax)[1] - 1 + 127, 0) - down, 1)
    scale = np.exp2(byte - 127.0)
    codes = (blocks / scale).astype(np.float32).astype(dtype).astype(np.float64)
    return np.moveaxis((codes * scale).reshape(v.shape), -1, axis)


WIDE = False


def mx_kscale(k):
    if not WIDE:
        return np.ones(k)
    levels = np.array([10, -10, 5, -5, 0])
    a = np.random.permutation(np.resize(levels, k // 512 * 4)).reshape(k // 512, 4)
    idx = np.arange(k)
    return np.exp2(a[idx // 512, idx % 128 // 32])


BF16 = ml_dtypes.bfloat16


def bf(x):
    return np.asarray(x, np.float32).astype(BF16)


def f64(x):
    return np.asarray(x).astype(np.float64)


B, D, H, F, C = 4096, 512, 1024, 512, 10


def blend_act(v):
    t = np.tanh(v)
    return np.where(v > 0, v * 0.9 + t * 0.1, t * 0.5)


def setup_inputs():
    s = mx_kscale(D)
    return {"x": bf(np.random.standard_normal((B, D)) * s),
            "W1": bf(np.random.standard_normal((D, H)) / np.sqrt(D) / s[:, None]),
            "b1": bf(np.random.standard_normal(H) * 0.3),
            "W2": bf(np.random.standard_normal((H, F)) * 1.5 / np.sqrt(H)),
            "b2": bf(np.random.standard_normal(F) * 0.3)}


def reference(x, W1, b1, W2, b2):
    h = blend_act((mxq(f64(x), 1, "e4m3") @ mxq(f64(W1), 0, "e4m3")) + f64(b1))
    return np.maximum((mxq(h, 1, "e4m3") @ mxq(f64(W2), 0, "e4m3")) + f64(b2), 0.0)

@@ -1,0 +1,219 @@
+from contextlib import ExitStack
+
+import concourse.mybir as mybir
+from concourse.masks import make_identity
+
+F32 = mybir.dt.float32
+BF16 = mybir.dt.bfloat16
+U32 = mybir.dt.uint32
+U8 = mybir.dt.uint8
+FP8X4 = mybir.dt.float8_e4m3fn_x4
+ACT = mybir.ActivationFunctionType
+ALU = mybir.AluOpType
+
+P = 128
+B, D, H, F = 4096, 512, 1024, 512
+CH = 512
+NCH = B // CH
+NJ = H // P
+FLOPS = 2 * B * D * H + 2 * B * H * F
+
+NV = 256
+RELU_ON = "gpsimd"
+
+
+def tile_complexnn_pa_kernel(tc, x, W1, b1, W2, b2, out):
+    nc = tc.nc
+    with ExitStack() as ctx:
+        const = ctx.enter_context(tc.tile_pool(name="const", bufs=1))
+        xin = ctx.enter_context(tc.tile_pool(name="xin", bufs=NCH))
+        xq = ctx.enter_context(tc.tile_pool(name="xq", bufs=2))
+        act = ctx.enter_context(tc.tile_pool(name="act", bufs=3))
+        hq = ctx.enter_context(tc.tile_pool(name="hq", bufs=4))
+        outp = ctx.enter_context(tc.tile_pool(name="outp", bufs=6))
+        psx = ctx.enter_context(tc.psum_pool(name="psx", bufs=2))
+        ps1 = ctx.enter_context(tc.psum_pool(name="ps1", bufs=4))
+        ps2 = ctx.enter_context(tc.psum_pool(name="ps2", bufs=2))
+
+        w1_raw = const.tile([P, 4, H], BF16)
+        for u in range(2):
+            nc.sync.dma_start(
+                out=w1_raw[:, 2 * u : 2 * u + 2, :],
+                in_=W1[256 * u : 256 * u + 256, :].rearrange("(q e) c -> q e c", e=2),
+            )
+        x_tiles = []
+        x_view = x.rearrange("(c p q) d -> c p (q d)", p=P, q=4)
+
+        def load_x(c):
+            x_t = xin.tile([P, 4 * D], BF16)
+            nc.sync.dma_start(out=x_t[:], in_=x_view[c])
+            x_tiles.append(x_t)
+
+        load_x(0)
+        b1_bf = const.tile([P, NJ], BF16)
+        with nc.allow_non_contiguous_dma(reason="1024 bias values, one per partition and hidden tile"):
+            nc.scalar.dma_start(out=b1_bf[:], in_=b1.rearrange("(j m) -> m j", m=P))
+        w2_raw = const.tile([P, NJ, F], BF16)
+        nc.sync.dma_start(out=w2_raw[:], in_=W2.rearrange("(j m) f -> m j f", m=P))
+        load_x(1)
+        b2_bf = const.tile([P, F], BF16)
+        nc.sync.dma_start(out=b2_bf[:], in_=b2.partition_broadcast(P))
+        for c in range(2, NCH):
+            load_x(c)
+
+        ident = const.tile([P, P], F32)
+        make_identity(nc, ident[:])
+
+        b1_f = const.tile([P, NJ], F32)
+        nc.vector.tensor_copy(out=b1_f[:], in_=b1_bf[:])
+        b1_s = const.tile([P, NJ], F32)
+        nc.vector.tensor_scalar_mul(out=b1_s[:], in0=b1_bf[:], scalar1=1.8)
+        b2_f = const.tile([P, F], F32)
+
+        w1_g = const.tile([P, H, 4], BF16, align_bytes=64)
+        w1_c = const.tile([P, H], U32, align_bytes=64)
+        w1_s = const.tile([P, H], U8, align_bytes=64)
+        w2_g = const.tile([P, 2, F, 4], BF16, align_bytes=64)
+        w2_c = const.tile([P, 2, F], U32, align_bytes=64)
+        w2_s = const.tile([P, 2, F], U8, align_bytes=64)
+
+        def regroup(eng_copy, dst, src):
+            eng_copy(
+                out=dst.rearrange("p (c i) t -> p c t i", i=4),
+                in_=src.rearrange("p t (c i) -> p c t i", i=4),
+            )
+
+        def prep_w1():
+            regroup(nc.vector.tensor_copy, w1_g[:, 0:512, :], w1_raw[:, :, 0:512])
+            regroup(nc.scalar.copy, w1_g[:, 512:1024, :], w1_raw[:, :, 512:1024])
+            for g in range(2):
+                cols = slice(512 * g, 512 * g + 512)
+                nc.vector.quantize_mx(
+                    out=w1_c[:, cols].bitcast(FP8X4),
+                    scales=w1_s[:, cols],
+                    in_=w1_g[:, cols, :].rearrange("p c t -> p (c t)"),
+                )
+
+        def prep_w2():
+            for g in range(2):
+                regroup(nc.vector.tensor_copy, w2_g[:, g, :, :], w2_raw[:, 4 * g : 4 * g + 4, :])
+            for g in range(2):
+                nc.vector.quantize_mx(
+                    out=w2_c[:, g, :].bitcast(FP8X4),
+                    scales=w2_s[:, g, :],
+                    in_=w2_g[:, g, :, :].rearrange("p c t -> p (c t)"),
+                )
+            nc.vector.tensor_copy(out=b2_f[:], in_=b2_bf[:])
+
+        x_codes = {}
+
+        def prep_x(c):
+            xw = x_tiles[c][:].bitcast(F32)
+            xg = xq.tile([P, 4 * CH], BF16, align_bytes=64)
+            xg_w = xg[:].bitcast(F32).rearrange("p (n u) -> p n u", u=2)
+            for b in range(2):
+                xt = psx.tile([P, 2, 256], F32)
+                for qq in range(2):
+                    q = 2 * b + qq
+                    for u in range(2):
+                        nc.tensor.transpose(
+                            xt[:, u, qq * P : (qq + 1) * P],
+                            xw[:, q * 256 + u * P : q * 256 + (u + 1) * P],
+                            ident[:],
+                        )
+                nc.scalar.copy(
+                    out=xg_w[:, b * 256 : (b + 1) * 256, :],
+                    in_=xt[:].rearrange("p u n -> p n u"),
+                )
+            xc = xq.tile([P, CH], U32, align_bytes=64)
+            xs = xq.tile([P, CH], U8, align_bytes=64)
+            nc.vector.quantize_mx(out=xc[:].bitcast(FP8X4), scales=xs[:], in_=xg[:])
+            x_codes[c] = (xc, xs)
+
+        h_codes = {}
+
+        def layer1(c, g):
+            xc, xs = x_codes[c]
+            tt = act.tile([P, 4, CH], F32)
+            wt = act.tile([P, 4, CH], F32)
+            for t in range(4):
+                j = 4 * g + t
+                acc = ps1.tile([P, CH], F32)
+                nc.tensor.matmul_mx(
+                    out=acc[:],
+                    lhsT=w1_c[:, j * P : (j + 1) * P].bitcast(FP8X4),
+                    lhsT_scale=w1_s[:, j * P : (j + 1) * P],
+                    rhs=xc[:].bitcast(FP8X4),
+                    rhs_scale=xs[:],
+                    start=True,
+                    stop=True,
+                )
+                nc.scalar.activation(
+                    out=tt[:, t, :], in_=acc[:], func=ACT.Tanh, bias=b1_f[:, j : j + 1], scale=1.0
+                )
+                nc.vector.scalar_tensor_tensor(
+                    out=wt[:, t, :], in0=tt[:, t, :], scalar=-4.0 / 9.0, in1=acc[:],
+                    op0=ALU.mult, op1=ALU.add,
+                )
+                nc.scalar.activation(
+                    out=wt[:, t, :], in_=wt[:, t, :], func=ACT.Relu, bias=b1_s[:, j : j + 1], scale=1.8
+                )
+            hg = hq.tile([P, 4 * CH], BF16, align_bytes=64)
+            hg_v = hg[:].rearrange("p (n t) -> p n t", t=4)
+            if NV > 0:
+                nc.vector.tensor_tensor(
+                    out=hg_v[:, 0:NV, :],
+                    in0=wt[:, :, 0:NV].rearrange("p t n -> p n t"),
+                    in1=tt[:, :, 0:NV].rearrange("p t n -> p n t"),
+                    op=ALU.add,
+                )
+            if NV < CH:
+                nc.gpsimd.tensor_tensor(
+                    out=hg_v[:, NV:CH, :],
+                    in0=wt[:, :, NV:CH].rearrange("p t n -> p n t"),
+                    in1=tt[:, :, NV:CH].rearrange("p t n -> p n t"),
+                    op=ALU.add,
+                )
+            hc = hq.tile([P, CH], U32, align_bytes=64)
+            hs = hq.tile([P, CH], U8, align_bytes=64)
+            nc.vector.quantize_mx(out=hc[:].bitcast(FP8X4), scales=hs[:], in_=hg[:])
+            h_codes[(c, g)] = (hc, hs)
+
+        out_view = out.rearrange("(c p q) f -> c q p f", p=P, q=4)
+
+        def layer2(c):
+            for q in range(4):
+                acc2 = ps2.tile([P, F], F32)
+                for g in range(2):
+                    hc, hs = h_codes[(c, g)]
+                    nc.tensor.matmul_mx(
+                        out=acc2[:],
+                        lhsT=hc[:, q * P : (q + 1) * P].bitcast(FP8X4),
+                        lhsT_scale=hs[:, q * P : (q + 1) * P],
+                        rhs=w2_c[:, g, :].bitcast(FP8X4),
+                        rhs_scale=w2_s[:, g, :],
+                        start=(g == 0),
+                        stop=(g == 1),
+                    )
+                o_t = outp.tile([P, F], F32)
+                nc.vector.scalar_tensor_tensor(
+                    out=o_t[:], in0=acc2[:], scalar=0.5, in1=b2_f[:], op0=ALU.mult, op1=ALU.add
+                )
+                if RELU_ON == "gpsimd":
+                    nc.gpsimd.tensor_scalar(
+                        out=o_t[:], in0=o_t[:], scalar1=0.0, scalar2=0.0, op0=ALU.max, op1=ALU.add
+                    )
+                else:
+                    nc.vector.tensor_scalar_max(out=o_t[:], in0=o_t[:], scalar1=0.0)
+                nc.sync.dma_start(out=out_view[c, q], in_=o_t[:])
+
+        prep_w1()
+        prep_x(0)
+        for c in range(NCH):
+            layer1(c, 0)
+            if c == 0:
+                prep_w2()
+            if c + 1 < NCH:
+                prep_x(c + 1)
+            layer1(c, 1)
+            layer2(c)

@@ -18,8 +18,8 @@ NCH = B // CH
 NJ = H // P
 FLOPS = 2 * B * D * H + 2 * B * H * F
 
-NV = 256
-RELU_ON = "gpsimd"
+NV = 512
+RELU_ON = "scalar"
 
 
 def tile_complexnn_pa_kernel(tc, x, W1, b1, W2, b2, out):
@@ -36,11 +36,6 @@ def tile_complexnn_pa_kernel(tc, x, W1, b1, W2, b2, out):
         ps2 = ctx.enter_context(tc.psum_pool(name="ps2", bufs=2))
 
         w1_raw = const.tile([P, 4, H], BF16)
-        for u in range(2):
-            nc.sync.dma_start(
-                out=w1_raw[:, 2 * u : 2 * u + 2, :],
-                in_=W1[256 * u : 256 * u + 256, :].rearrange("(q e) c -> q e c", e=2),
-            )
         x_tiles = []
         x_view = x.rearrange("(c p q) d -> c p (q d)", p=P, q=4)
 
@@ -50,6 +45,14 @@ def tile_complexnn_pa_kernel(tc, x, W1, b1, W2, b2, out):
             x_tiles.append(x_t)
 
         load_x(0)
+        for g in range(2):
+            for u in range(2):
+                nc.sync.dma_start(
+                    out=w1_raw[:, 2 * u : 2 * u + 2, 512 * g : 512 * g + 512],
+                    in_=W1[256 * u : 256 * u + 256, 512 * g : 512 * g + 512].rearrange(
+                        "(q e) c -> q e c", e=2
+                    ),
+                )
         b1_bf = const.tile([P, NJ], BF16)
         with nc.allow_non_contiguous_dma(reason="1024 bias values, one per partition and hidden tile"):
             nc.scalar.dma_start(out=b1_bf[:], in_=b1.rearrange("(j m) -> m j", m=P))
@@ -203,6 +206,8 @@ def tile_complexnn_pa_kernel(tc, x, W1, b1, W2, b2, out):
                     nc.gpsimd.tensor_scalar(
                         out=o_t[:], in0=o_t[:], scalar1=0.0, scalar2=0.0, op0=ALU.max, op1=ALU.add
                     )
+                elif RELU_ON == "scalar":
+                    nc.scalar.activation(out=o_t[:], in_=o_t[:], func=ACT.Relu)
                 else:
                     nc.vector.tensor_scalar_max(out=o_t[:], in0=o_t[:], scalar1=0.0)
                 nc.sync.dma_start(out=out_view[c, q], in_=o_t[:])

@@ -18,7 +18,6 @@ NCH = B // CH
 NJ = H // P
 FLOPS = 2 * B * D * H + 2 * B * H * F
 
-NV = 512
 RELU_ON = "scalar"
 
 
@@ -155,28 +154,19 @@ def tile_complexnn_pa_kernel(tc, x, W1, b1, W2, b2, out):
                     out=tt[:, t, :], in_=acc[:], func=ACT.Tanh, bias=b1_f[:, j : j + 1], scale=1.0
                 )
                 nc.vector.scalar_tensor_tensor(
-                    out=wt[:, t, :], in0=tt[:, t, :], scalar=-4.0 / 9.0, in1=acc[:],
+                    out=wt[:, t, :], in0=tt[:, t, :], scalar=1.0 / 9.0, in1=acc[:],
                     op0=ALU.mult, op1=ALU.add,
                 )
                 nc.scalar.activation(
-                    out=wt[:, t, :], in_=wt[:, t, :], func=ACT.Relu, bias=b1_s[:, j : j + 1], scale=1.8
+                    out=wt[:, t, :], in_=wt[:, t, :], func=ACT.Identity, bias=b1_s[:, j : j + 1], scale=1.8
                 )
             hg = hq.tile([P, 4 * CH], BF16, align_bytes=64)
-            hg_v = hg[:].rearrange("p (n t) -> p n t", t=4)
-            if NV > 0:
-                nc.vector.tensor_tensor(
-                    out=hg_v[:, 0:NV, :],
-                    in0=wt[:, :, 0:NV].rearrange("p t n -> p n t"),
-                    in1=tt[:, :, 0:NV].rearrange("p t n -> p n t"),
-                    op=ALU.add,
-                )
-            if NV < CH:
-                nc.gpsimd.tensor_tensor(
-                    out=hg_v[:, NV:CH, :],
-                    in0=wt[:, :, NV:CH].rearrange("p t n -> p n t"),
-                    in1=tt[:, :, NV:CH].rearrange("p t n -> p n t"),
-                    op=ALU.add,
-                )
+            nc.vector.tensor_tensor(
+                out=hg[:].rearrange("p (c i t) -> p c t i", i=4, t=4),
+                in0=wt[:].rearrange("p t (c i) -> p c t i", i=4),
+                in1=tt[:].rearrange("p t (c i) -> p c t i", i=4),
+                op=ALU.max,
+            )
             hc = hq.tile([P, CH], U32, align_bytes=64)
             hs = hq.tile([P, CH], U8, align_bytes=64)
             nc.vector.quantize_mx(out=hc[:].bitcast(FP8X4), scales=hs[:], in_=hg[:])

@@ -157,9 +157,15 @@ def tile_complexnn_pa_kernel(tc, x, W1, b1, W2, b2, out):
                     out=wt[:, t, :], in0=tt[:, t, :], scalar=1.0 / 9.0, in1=acc[:],
                     op0=ALU.mult, op1=ALU.add,
                 )
-                nc.scalar.activation(
-                    out=wt[:, t, :], in_=wt[:, t, :], func=ACT.Identity, bias=b1_s[:, j : j + 1], scale=1.8
-                )
+                if t % 2 == 1:
+                    nc.gpsimd.tensor_scalar(
+                        out=wt[:, t, :], in0=wt[:, t, :], scalar1=1.8, scalar2=b1_s[:, j : j + 1],
+                        op0=ALU.mult, op1=ALU.add,
+                    )
+                else:
+                    nc.scalar.activation(
+                        out=wt[:, t, :], in_=wt[:, t, :], func=ACT.Identity, bias=b1_s[:, j : j + 1], scale=1.8
+                    )
             hg = hq.tile([P, 4 * CH], BF16, align_bytes=64)
             nc.vector.tensor_tensor(
                 out=hg[:].rearrange("p (c i t) -> p c t i", i=4, t=4),

@@ -16,9 +16,10 @@ B, D, H, F = 4096, 512, 1024, 512
 CH = 512
 NCH = B // CH
 NJ = H // P
+NG = 2 * NCH
 FLOPS = 2 * B * D * H + 2 * B * H * F
 
-RELU_ON = "scalar"
+GP_T = (1, 2, 3)
 
 
 def tile_complexnn_pa_kernel(tc, x, W1, b1, W2, b2, out):
@@ -28,21 +29,40 @@ def tile_complexnn_pa_kernel(tc, x, W1, b1, W2, b2, out):
         xin = ctx.enter_context(tc.tile_pool(name="xin", bufs=NCH))
         xq = ctx.enter_context(tc.tile_pool(name="xq", bufs=2))
         act = ctx.enter_context(tc.tile_pool(name="act", bufs=3))
-        hq = ctx.enter_context(tc.tile_pool(name="hq", bufs=4))
-        outp = ctx.enter_context(tc.tile_pool(name="outp", bufs=6))
-        psx = ctx.enter_context(tc.psum_pool(name="psx", bufs=2))
+        hgp = ctx.enter_context(tc.tile_pool(name="hgp", bufs=2))
+        hcp = ctx.enter_context(tc.tile_pool(name="hcp", bufs=5))
+        yp = ctx.enter_context(tc.tile_pool(name="yp", bufs=3))
+        outp = ctx.enter_context(tc.tile_pool(name="outp", bufs=3))
         ps1 = ctx.enter_context(tc.psum_pool(name="ps1", bufs=4))
-        ps2 = ctx.enter_context(tc.psum_pool(name="ps2", bufs=2))
+        psA = ctx.enter_context(tc.psum_pool(name="psA", bufs=2))
+        psT = ctx.enter_context(tc.psum_pool(name="psT", bufs=1))
+        psX = ctx.enter_context(tc.psum_pool(name="psX", bufs=1))
+        ctx.enter_context(tc.manual_schedule())
 
-        w1_raw = const.tile([P, 4, H], BF16)
-        x_tiles = []
+        def bank(pool):
+            if pool is ps1:
+                return ps1.tile([P, 512], F32, name="acc", tag="acc")
+            if pool is psA:
+                return psA.tile([P, 512], F32, name="acc2", tag="acc2")
+            if pool is psT:
+                return psT.tile([P, 512], F32, name="tr", tag="tr")
+            return psX.tile([P, 512], F32, name="xt", tag="xt")
+
+        b1_bf = const.tile([P, NJ], BF16)
+        b2_bf = const.tile([P, 4], BF16)
+        with nc.allow_non_contiguous_dma(reason="bias values, one per partition and tile"):
+            nc.scalar.dma_start(out=b1_bf[:], in_=b1.rearrange("(j m) -> m j", m=P))
+            nc.scalar.dma_start(out=b2_bf[:], in_=b2.rearrange("(j m) -> m j", m=P))
         x_view = x.rearrange("(c p q) d -> c p (q d)", p=P, q=4)
+        x_tiles = []
 
         def load_x(c):
             x_t = xin.tile([P, 4 * D], BF16)
             nc.sync.dma_start(out=x_t[:], in_=x_view[c])
             x_tiles.append(x_t)
 
+        w1_raw = const.tile([P, 4, H], BF16)
+        w2_raw = const.tile([P, NJ, F], BF16)
         load_x(0)
         for g in range(2):
             for u in range(2):
@@ -52,14 +72,8 @@ def tile_complexnn_pa_kernel(tc, x, W1, b1, W2, b2, out):
                         "(q e) c -> q e c", e=2
                     ),
                 )
-        b1_bf = const.tile([P, NJ], BF16)
-        with nc.allow_non_contiguous_dma(reason="1024 bias values, one per partition and hidden tile"):
-            nc.scalar.dma_start(out=b1_bf[:], in_=b1.rearrange("(j m) -> m j", m=P))
-        w2_raw = const.tile([P, NJ, F], BF16)
-        nc.sync.dma_start(out=w2_raw[:], in_=W2.rearrange("(j m) f -> m j f", m=P))
         load_x(1)
-        b2_bf = const.tile([P, F], BF16)
-        nc.sync.dma_start(out=b2_bf[:], in_=b2.partition_broadcast(P))
+        nc.sync.dma_start(out=w2_raw[:], in_=W2.rearrange("(j m) f -> m j f", m=P))
         for c in range(2, NCH):
             load_x(c)
 
@@ -67,10 +81,8 @@ def tile_complexnn_pa_kernel(tc, x, W1, b1, W2, b2, out):
         make_identity(nc, ident[:])
 
         b1_f = const.tile([P, NJ], F32)
-        nc.vector.tensor_copy(out=b1_f[:], in_=b1_bf[:])
         b1_s = const.tile([P, NJ], F32)
-        nc.vector.tensor_scalar_mul(out=b1_s[:], in0=b1_bf[:], scalar1=1.8)
-        b2_f = const.tile([P, F], F32)
+        b2_c = const.tile([P, 4], F32)
 
         w1_g = const.tile([P, H, 4], BF16, align_bytes=64)
         w1_c = const.tile([P, H], U32, align_bytes=64)
@@ -79,142 +91,255 @@ def tile_complexnn_pa_kernel(tc, x, W1, b1, W2, b2, out):
         w2_c = const.tile([P, 2, F], U32, align_bytes=64)
         w2_s = const.tile([P, 2, F], U8, align_bytes=64)
 
-        def regroup(eng_copy, dst, src):
-            eng_copy(
+        def regroup_v(dst, src):
+            nc.vector.tensor_copy(
                 out=dst.rearrange("p (c i) t -> p c t i", i=4),
                 in_=src.rearrange("p t (c i) -> p c t i", i=4),
             )
 
-        def prep_w1():
-            regroup(nc.vector.tensor_copy, w1_g[:, 0:512, :], w1_raw[:, :, 0:512])
-            regroup(nc.scalar.copy, w1_g[:, 512:1024, :], w1_raw[:, :, 512:1024])
-            for g in range(2):
-                cols = slice(512 * g, 512 * g + 512)
-                nc.vector.quantize_mx(
-                    out=w1_c[:, cols].bitcast(FP8X4),
-                    scales=w1_s[:, cols],
-                    in_=w1_g[:, cols, :].rearrange("p c t -> p (c t)"),
-                )
+        def regroup_g(dst, src):
+            nc.gpsimd.tensor_scalar(
+                out=dst, in0=src.rearrange("p t c -> p c t"), scalar1=1.0, scalar2=0.0,
+                op0=ALU.mult, op1=ALU.add,
+            )
 
-        def prep_w2():
-            for g in range(2):
-                regroup(nc.vector.tensor_copy, w2_g[:, g, :, :], w2_raw[:, 4 * g : 4 * g + 4, :])
-            for g in range(2):
-                nc.vector.quantize_mx(
-                    out=w2_c[:, g, :].bitcast(FP8X4),
-                    scales=w2_s[:, g, :],
-                    in_=w2_g[:, g, :, :].rearrange("p c t -> p (c t)"),
-                )
-            nc.vector.tensor_copy(out=b2_f[:], in_=b2_bf[:])
+        def quant_w1(c0, c1):
+            nc.vector.quantize_mx(
+                out=w1_c[:, c0:c1].bitcast(FP8X4),
+                scales=w1_s[:, c0:c1],
+                in_=w1_g[:, c0:c1, :].rearrange("p c t -> p (c t)"),
+            )
 
+        def quant_w2(g):
+            nc.vector.quantize_mx(
+                out=w2_c[:, g, :].bitcast(FP8X4),
+                scales=w2_s[:, g, :],
+                in_=w2_g[:, g, :, :].rearrange("p c t -> p (c t)"),
+            )
+
+        xgs = {}
         x_codes = {}
 
-        def prep_x(c):
+        def x_half(c, b, pool):
+            if b == 0:
+                xg = xq.tile([P, 4 * CH], BF16, align_bytes=64)
+                xgs[c] = xg
             xw = x_tiles[c][:].bitcast(F32)
-            xg = xq.tile([P, 4 * CH], BF16, align_bytes=64)
-            xg_w = xg[:].bitcast(F32).rearrange("p (n u) -> p n u", u=2)
-            for b in range(2):
-                xt = psx.tile([P, 2, 256], F32)
-                for qq in range(2):
-                    q = 2 * b + qq
-                    for u in range(2):
-                        nc.tensor.transpose(
-                            xt[:, u, qq * P : (qq + 1) * P],
-                            xw[:, q * 256 + u * P : q * 256 + (u + 1) * P],
-                            ident[:],
-                        )
-                nc.scalar.copy(
-                    out=xg_w[:, b * 256 : (b + 1) * 256, :],
-                    in_=xt[:].rearrange("p u n -> p n u"),
-                )
+            xt = bank(pool)
+            for qq in range(2):
+                q = 2 * b + qq
+                for u in range(2):
+                    nc.tensor.transpose(
+                        xt[:, u * 256 + qq * P : u * 256 + (qq + 1) * P],
+                        xw[:, q * 256 + u * P : q * 256 + (u + 1) * P],
+                        ident[:],
+                    )
+            xg_w = xgs[c][:].bitcast(F32).rearrange("p (n u) -> p n u", u=2)
+            nc.scalar.copy(
+                out=xg_w[:, b * 256 : (b + 1) * 256, :],
+                in_=xt[:].rearrange("p (u n) -> p n u", u=2),
+            )
+
+        def x_quant(c):
             xc = xq.tile([P, CH], U32, align_bytes=64)
             xs = xq.tile([P, CH], U8, align_bytes=64)
-            nc.vector.quantize_mx(out=xc[:].bitcast(FP8X4), scales=xs[:], in_=xg[:])
+            nc.vector.quantize_mx(out=xc[:].bitcast(FP8X4), scales=xs[:], in_=xgs[c][:])
             x_codes[c] = (xc, xs)
 
+        tts = {}
+        wts = {}
+        accs = {}
+        hgs = {}
         h_codes = {}
 
-        def layer1(c, g):
-            xc, xs = x_codes[c]
-            tt = act.tile([P, 4, CH], F32)
-            wt = act.tile([P, 4, CH], F32)
-            for t in range(4):
-                j = 4 * g + t
-                acc = ps1.tile([P, CH], F32)
-                nc.tensor.matmul_mx(
-                    out=acc[:],
-                    lhsT=w1_c[:, j * P : (j + 1) * P].bitcast(FP8X4),
-                    lhsT_scale=w1_s[:, j * P : (j + 1) * P],
-                    rhs=xc[:].bitcast(FP8X4),
-                    rhs_scale=xs[:],
-                    start=True,
-                    stop=True,
-                )
-                nc.scalar.activation(
-                    out=tt[:, t, :], in_=acc[:], func=ACT.Tanh, bias=b1_f[:, j : j + 1], scale=1.0
-                )
-                nc.vector.scalar_tensor_tensor(
-                    out=wt[:, t, :], in0=tt[:, t, :], scalar=1.0 / 9.0, in1=acc[:],
+        def l1_tanh(s, t):
+            xc, xs = x_codes[s // 2]
+            j = 4 * (s % 2) + t
+            if t == 0:
+                tt = act.tile([P, 4, CH], F32)
+                wt = act.tile([P, 4, CH], F32)
+                tts[s] = tt
+                wts[s] = wt
+            acc = bank(ps1)
+            accs[(s, t)] = acc
+            nc.tensor.matmul_mx(
+                out=acc[:],
+                lhsT=w1_c[:, j * P : (j + 1) * P].bitcast(FP8X4),
+                lhsT_scale=w1_s[:, j * P : (j + 1) * P],
+                rhs=xc[:].bitcast(FP8X4),
+                rhs_scale=xs[:],
+                start=True,
+                stop=True,
+            )
+            nc.scalar.activation(
+                out=tts[s][:, t, :], in_=acc[:], func=ACT.Tanh, bias=b1_f[:, j : j + 1], scale=1.0
+            )
+
+        def u_op(s, t):
+            nc.vector.scalar_tensor_tensor(
+                out=wts[s][:, t, :], in0=tts[s][:, t, :], scalar=1.0 / 9.0, in1=accs[(s, t)][:],
+                op0=ALU.mult, op1=ALU.add,
+            )
+
+        def y_op(s, t):
+            j = 4 * (s % 2) + t
+            if t in GP_T:
+                nc.gpsimd.tensor_scalar(
+                    out=wts[s][:, t, :], in0=wts[s][:, t, :], scalar1=1.8, scalar2=b1_s[:, j : j + 1],
                     op0=ALU.mult, op1=ALU.add,
                 )
-                if t % 2 == 1:
-                    nc.gpsimd.tensor_scalar(
-                        out=wt[:, t, :], in0=wt[:, t, :], scalar1=1.8, scalar2=b1_s[:, j : j + 1],
-                        op0=ALU.mult, op1=ALU.add,
-                    )
-                else:
-                    nc.scalar.activation(
-                        out=wt[:, t, :], in_=wt[:, t, :], func=ACT.Identity, bias=b1_s[:, j : j + 1], scale=1.8
-                    )
-            hg = hq.tile([P, 4 * CH], BF16, align_bytes=64)
+            else:
+                nc.scalar.activation(
+                    out=wts[s][:, t, :], in_=wts[s][:, t, :], func=ACT.Identity,
+                    bias=b1_s[:, j : j + 1], scale=1.8,
+                )
+
+        def h_max(s):
+            hg = hgp.tile([P, 4 * CH], BF16, align_bytes=64)
+            hgs[s] = hg
             nc.vector.tensor_tensor(
                 out=hg[:].rearrange("p (c i t) -> p c t i", i=4, t=4),
-                in0=wt[:].rearrange("p t (c i) -> p c t i", i=4),
-                in1=tt[:].rearrange("p t (c i) -> p c t i", i=4),
+                in0=wts[s][:].rearrange("p t (c i) -> p c t i", i=4),
+                in1=tts[s][:].rearrange("p t (c i) -> p c t i", i=4),
                 op=ALU.max,
             )
-            hc = hq.tile([P, CH], U32, align_bytes=64)
-            hs = hq.tile([P, CH], U8, align_bytes=64)
-            nc.vector.quantize_mx(out=hc[:].bitcast(FP8X4), scales=hs[:], in_=hg[:])
-            h_codes[(c, g)] = (hc, hs)
 
-        out_view = out.rearrange("(c p q) f -> c q p f", p=P, q=4)
+        def h_quant(s):
+            hc = hcp.tile([P, CH], U32, align_bytes=64)
+            hs = hcp.tile([P, CH], U8, align_bytes=64)
+            nc.vector.quantize_mx(out=hc[:].bitcast(FP8X4), scales=hs[:], in_=hgs[s][:])
+            h_codes[s] = (hc, hs)
 
-        def layer2(c):
-            for q in range(4):
-                acc2 = ps2.tile([P, F], F32)
-                for g in range(2):
-                    hc, hs = h_codes[(c, g)]
-                    nc.tensor.matmul_mx(
-                        out=acc2[:],
-                        lhsT=hc[:, q * P : (q + 1) * P].bitcast(FP8X4),
-                        lhsT_scale=hs[:, q * P : (q + 1) * P],
-                        rhs=w2_c[:, g, :].bitcast(FP8X4),
-                        rhs_scale=w2_s[:, g, :],
-                        start=(g == 0),
-                        stop=(g == 1),
-                    )
-                o_t = outp.tile([P, F], F32)
-                nc.vector.scalar_tensor_tensor(
-                    out=o_t[:], in0=acc2[:], scalar=0.5, in1=b2_f[:], op0=ALU.mult, op1=ALU.add
+        out_view = out.rearrange("(c p q) f -> c p q f", p=P, q=4)
+        ys = {}
+
+        def l2_pass(acc2, c, fc, g):
+            hc, hs = h_codes[2 * c + g]
+            nc.tensor.matmul_mx(
+                out=acc2[:],
+                lhsT=w2_c[:, g, fc * P : (fc + 1) * P].bitcast(FP8X4),
+                lhsT_scale=w2_s[:, g, fc * P : (fc + 1) * P],
+                rhs=hc[:].bitcast(FP8X4),
+                rhs_scale=hs[:],
+                start=(g == 0),
+                stop=(g == 1),
+            )
+
+        def l2_bias(acc2, c, fc, on_vector):
+            y_t = yp.tile([P, CH], F32)
+            ys[(c, fc)] = y_t
+            if on_vector:
+                nc.vector.tensor_scalar(
+                    out=y_t[:], in0=acc2[:], scalar1=0.5, scalar2=b2_c[:, fc : fc + 1],
+                    op0=ALU.mult, op1=ALU.add,
                 )
-                if RELU_ON == "gpsimd":
-                    nc.gpsimd.tensor_scalar(
-                        out=o_t[:], in0=o_t[:], scalar1=0.0, scalar2=0.0, op0=ALU.max, op1=ALU.add
-                    )
-                elif RELU_ON == "scalar":
-                    nc.scalar.activation(out=o_t[:], in_=o_t[:], func=ACT.Relu)
-                else:
-                    nc.vector.tensor_scalar_max(out=o_t[:], in0=o_t[:], scalar1=0.0)
-                nc.sync.dma_start(out=out_view[c, q], in_=o_t[:])
+            else:
+                nc.scalar.activation(
+                    out=y_t[:], in_=acc2[:], func=ACT.Identity, bias=b2_c[:, fc : fc + 1], scale=0.5
+                )
 
-        prep_w1()
-        prep_x(0)
-        for c in range(NCH):
-            layer1(c, 0)
-            if c == 0:
-                prep_w2()
-            if c + 1 < NCH:
-                prep_x(c + 1)
-            layer1(c, 1)
-            layer2(c)
+        def job_l(c, fc):
+            acc2 = bank(psA)
+            l2_pass(acc2, c, fc, 0)
+            l2_pass(acc2, c, fc, 1)
+            l2_bias(acc2, c, fc, False)
+
+        def job_t(c, fc, pool, on_vector):
+            y_t = ys[(c, fc)]
+            tr = bank(pool)
+            for q in range(4):
+                nc.tensor.transpose(tr[:, q * P : (q + 1) * P], y_t[:, q * P : (q + 1) * P], ident[:])
+            o_t = outp.tile([P, 4, P], F32)
+            if on_vector:
+                nc.vector.tensor_scalar_max(
+                    out=o_t[:].rearrange("p q f -> p (q f)"), in0=tr[:], scalar1=0.0
+                )
+            else:
+                nc.scalar.activation(
+                    out=o_t[:].rearrange("p q f -> p (q f)"), in_=tr[:], func=ACT.Relu
+                )
+            nc.sync.dma_start(out=out_view[c][:, :, fc * P : (fc + 1) * P], in_=o_t[:])
+
+        regroup_v(w1_g[:, 0:512, :], w1_raw[:, :, 0:512])
+        regroup_g(w1_g[:, 512:768, :], w1_raw[:, :, 512:768])
+        regroup_g(w1_g[:, 768:1024, :], w1_raw[:, :, 768:1024])
+        quant_w1(0, 512)
+        x_half(0, 0, psX)
+        x_half(0, 1, psT)
+        x_quant(0)
+        nc.vector.tensor_copy(out=b1_f[:], in_=b1_bf[:])
+        nc.vector.tensor_scalar_mul(out=b1_s[:], in0=b1_bf[:], scalar1=1.8)
+        nc.vector.tensor_copy(out=b2_c[:], in_=b2_bf[:])
+        l1_tanh(0, 0)
+        l1_tanh(0, 1)
+        x_half(1, 0, psX)
+        l1_tanh(0, 2)
+        l1_tanh(0, 3)
+        x_half(1, 1, psT)
+        quant_w1(512, 768)
+
+        done = [0, 0]
+        n_main = 4 * (NCH - 1)
+
+        def slot_l(s):
+            n = done[0]
+            if n < n_main and s >= 2 * (n // 4) + 3:
+                job_l(n // 4, n % 4)
+                done[0] = n + 1
+
+        def slot_t(keep, pool):
+            n = done[1]
+            if n < done[0] - keep:
+                job_t(n // 4, n % 4, pool, False)
+                done[1] = n + 1
+
+        for s in range(NG):
+            for t in range(4):
+                u_op(s, t)
+                if s == 0 and t == 1:
+                    quant_w1(768, 1024)
+                if s + 1 < NG:
+                    l1_tanh(s + 1, t)
+                y_op(s, t)
+                if t == 0 and s >= 2:
+                    h_quant(s - 2)
+                if t % 2 == 0:
+                    slot_l(s)
+                else:
+                    slot_t(1, psT)
+            if s < 2:
+                regroup_g(w2_g[:, s, :, :], w2_raw[:, 4 * s : 4 * s + 4, :])
+            if s + 4 < 2 * NCH:
+                x_half((s + 4) // 2, s % 2, psX)
+            if s == NG - 1:
+                for r in range(2):
+                    slot_l(s)
+                    slot_t(1, psT)
+            if s >= 1:
+                h_max(s - 1)
+            if s % 2 == 0 and (s + 2) // 2 < NCH:
+                x_quant((s + 2) // 2)
+            if s == 2:
+                quant_w2(0)
+                quant_w2(1)
+
+        last = NCH - 1
+        h_quant(NG - 2)
+        tail_acc = []
+        for fc in range(4):
+            acc2 = bank(ps1)
+            tail_acc.append(acc2)
+            l2_pass(acc2, last, fc, 0)
+        spare = [psT, psA, psX, psA]
+        n_spare = n_main - done[1]
+        for r in range(n_spare):
+            slot_t(0, spare[r % 4])
+        h_max(NG - 1)
+        h_quant(NG - 1)
+        for fc in range(4):
+            l2_pass(tail_acc[fc], last, fc, 1)
+            l2_bias(tail_acc[fc], last, fc, fc % 2 == 0)
+            if fc >= 1:
+                job_t(last, fc - 1, spare[n_spare % 4], fc % 2 == 1)
+                n_spare += 1
+        job_t(last, 3, spare[n_spare % 4], False)

@@ -19,14 +19,15 @@ NJ = H // P
 NG = 2 * NCH
 FLOPS = 2 * B * D * H + 2 * B * H * F
 
-GP_T = (1, 2, 3)
+GP_T = (0, 1, 3)
+VE_T = ()
 
 
 def tile_complexnn_pa_kernel(tc, x, W1, b1, W2, b2, out):
     nc = tc.nc
     with ExitStack() as ctx:
         const = ctx.enter_context(tc.tile_pool(name="const", bufs=1))
-        xin = ctx.enter_context(tc.tile_pool(name="xin", bufs=NCH))
+        xin = ctx.enter_context(tc.tile_pool(name="xin", bufs=2 * NCH))
         xq = ctx.enter_context(tc.tile_pool(name="xq", bufs=2))
         act = ctx.enter_context(tc.tile_pool(name="act", bufs=3))
         hgp = ctx.enter_context(tc.tile_pool(name="hgp", bufs=2))
@@ -50,32 +51,40 @@ def tile_complexnn_pa_kernel(tc, x, W1, b1, W2, b2, out):
 
         b1_bf = const.tile([P, NJ], BF16)
         b2_bf = const.tile([P, 4], BF16)
-        with nc.allow_non_contiguous_dma(reason="bias values, one per partition and tile"):
-            nc.scalar.dma_start(out=b1_bf[:], in_=b1.rearrange("(j m) -> m j", m=P))
-            nc.scalar.dma_start(out=b2_bf[:], in_=b2.rearrange("(j m) -> m j", m=P))
         x_view = x.rearrange("(c p q) d -> c p (q d)", p=P, q=4)
-        x_tiles = []
+        x_tiles = {}
 
-        def load_x(c):
-            x_t = xin.tile([P, 4 * D], BF16)
-            nc.sync.dma_start(out=x_t[:], in_=x_view[c])
-            x_tiles.append(x_t)
+        def load_x(c, b):
+            x_t = xin.tile([P, 2 * D], BF16)
+            nc.sync.dma_start(out=x_t[:], in_=x_view[c][:, b * 2 * D : (b + 1) * 2 * D])
+            x_tiles[(c, b)] = x_t
 
-        w1_raw = const.tile([P, 4, H], BF16)
+        w1_raw0 = const.tile([P, 4, 512], BF16)
+        w1_raw1 = const.tile([P, 4, 512], BF16)
         w2_raw = const.tile([P, NJ, F], BF16)
-        load_x(0)
-        for g in range(2):
+
+        def load_w1(g, dst):
             for u in range(2):
                 nc.sync.dma_start(
-                    out=w1_raw[:, 2 * u : 2 * u + 2, 512 * g : 512 * g + 512],
+                    out=dst[:, 2 * u : 2 * u + 2, :],
                     in_=W1[256 * u : 256 * u + 256, 512 * g : 512 * g + 512].rearrange(
                         "(q e) c -> q e c", e=2
                     ),
                 )
-        load_x(1)
+
+        load_x(0, 0)
+        load_w1(0, w1_raw0)
+        load_x(0, 1)
+        with nc.allow_non_contiguous_dma(reason="bias values, one per partition and tile"):
+            nc.sync.dma_start(out=b1_bf[:], in_=b1.rearrange("(j m) -> m j", m=P))
+            nc.sync.dma_start(out=b2_bf[:], in_=b2.rearrange("(j m) -> m j", m=P))
+        load_w1(1, w1_raw1)
+        load_x(1, 0)
+        load_x(1, 1)
         nc.sync.dma_start(out=w2_raw[:], in_=W2.rearrange("(j m) f -> m j f", m=P))
         for c in range(2, NCH):
-            load_x(c)
+            load_x(c, 0)
+            load_x(c, 1)
 
         ident = const.tile([P, P], F32)
         make_identity(nc, ident[:])
@@ -93,6 +102,12 @@ def tile_complexnn_pa_kernel(tc, x, W1, b1, W2, b2, out):
 
         def regroup_v(dst, src):
             nc.vector.tensor_copy(
+                out=dst.rearrange("p (c i) t -> p c t i", i=4),
+                in_=src.rearrange("p t (c i) -> p c t i", i=4),
+            )
+
+        def regroup_s(dst, src):
+            nc.scalar.copy(
                 out=dst.rearrange("p (c i) t -> p c t i", i=4),
                 in_=src.rearrange("p t (c i) -> p c t i", i=4),
             )
@@ -124,14 +139,13 @@ def tile_complexnn_pa_kernel(tc, x, W1, b1, W2, b2, out):
             if b == 0:
                 xg = xq.tile([P, 4 * CH], BF16, align_bytes=64)
                 xgs[c] = xg
-            xw = x_tiles[c][:].bitcast(F32)
+            xw = x_tiles[(c, b)][:].bitcast(F32)
             xt = bank(pool)
             for qq in range(2):
-                q = 2 * b + qq
                 for u in range(2):
                     nc.tensor.transpose(
                         xt[:, u * 256 + qq * P : u * 256 + (qq + 1) * P],
-                        xw[:, q * 256 + u * P : q * 256 + (u + 1) * P],
+                        xw[:, qq * 256 + u * P : qq * 256 + (u + 1) * P],
                         ident[:],
                     )
             xg_w = xgs[c][:].bitcast(F32).rearrange("p (n u) -> p n u", u=2)
@@ -140,11 +154,17 @@ def tile_complexnn_pa_kernel(tc, x, W1, b1, W2, b2, out):
                 in_=xt[:].rearrange("p (u n) -> p n u", u=2),
             )
 
-        def x_quant(c):
-            xc = xq.tile([P, CH], U32, align_bytes=64)
-            xs = xq.tile([P, CH], U8, align_bytes=64)
-            nc.vector.quantize_mx(out=xc[:].bitcast(FP8X4), scales=xs[:], in_=xgs[c][:])
-            x_codes[c] = (xc, xs)
+        def x_quant(c, b):
+            if b == 0:
+                xc = xq.tile([P, CH], U32, align_bytes=64)
+                xs = xq.tile([P, CH], U8, align_bytes=64)
+                x_codes[c] = (xc, xs)
+            xc, xs = x_codes[c]
+            nc.vector.quantize_mx(
+                out=xc[:, b * 256 : (b + 1) * 256].bitcast(FP8X4),
+                scales=xs[:, b * 256 : (b + 1) * 256],
+                in_=xgs[c][:, b * 1024 : (b + 1) * 1024],
+            )
 
         tts = {}
         wts = {}
@@ -183,7 +203,12 @@ def tile_complexnn_pa_kernel(tc, x, W1, b1, W2, b2, out):
 
         def y_op(s, t):
             j = 4 * (s % 2) + t
-            if t in GP_T:
+            if t in VE_T:
+                nc.vector.tensor_scalar(
+                    out=wts[s][:, t, :], in0=wts[s][:, t, :], scalar1=1.8, scalar2=b1_s[:, j : j + 1],
+                    op0=ALU.mult, op1=ALU.add,
+                )
+            elif t in GP_T:
                 nc.gpsimd.tensor_scalar(
                     out=wts[s][:, t, :], in0=wts[s][:, t, :], scalar1=1.8, scalar2=b1_s[:, j : j + 1],
                     op0=ALU.mult, op1=ALU.add,
@@ -260,13 +285,14 @@ def tile_complexnn_pa_kernel(tc, x, W1, b1, W2, b2, out):
                 )
             nc.sync.dma_start(out=out_view[c][:, :, fc * P : (fc + 1) * P], in_=o_t[:])
 
-        regroup_v(w1_g[:, 0:512, :], w1_raw[:, :, 0:512])
-        regroup_g(w1_g[:, 512:768, :], w1_raw[:, :, 512:768])
-        regroup_g(w1_g[:, 768:1024, :], w1_raw[:, :, 768:1024])
+        regroup_v(w1_g[:, 0:512, :], w1_raw0[:])
+        regroup_g(w1_g[:, 512:768, :], w1_raw1[:, :, 0:256])
+        regroup_g(w1_g[:, 768:1024, :], w1_raw1[:, :, 256:512])
         quant_w1(0, 512)
         x_half(0, 0, psX)
         x_half(0, 1, psT)
-        x_quant(0)
+        x_quant(0, 0)
+        x_quant(0, 1)
         nc.vector.tensor_copy(out=b1_f[:], in_=b1_bf[:])
         nc.vector.tensor_scalar_mul(out=b1_s[:], in0=b1_bf[:], scalar1=1.8)
         nc.vector.tensor_copy(out=b2_c[:], in_=b2_bf[:])
@@ -300,15 +326,16 @@ def tile_complexnn_pa_kernel(tc, x, W1, b1, W2, b2, out):
                     quant_w1(768, 1024)
                 if s + 1 < NG:
                     l1_tanh(s + 1, t)
-                y_op(s, t)
-                if t == 0 and s >= 2:
-                    h_quant(s - 2)
-                if t % 2 == 0:
+                if t not in VE_T:
+                    y_op(s, t)
+                if t == 0:
                     slot_l(s)
-                else:
+                if t == 1:
                     slot_t(1, psT)
+            slot_l(s)
+            slot_t(1, psT)
             if s < 2:
-                regroup_g(w2_g[:, s, :, :], w2_raw[:, 4 * s : 4 * s + 4, :])
+                regroup_s(w2_g[:, s, :, :], w2_raw[:, 4 * s : 4 * s + 4, :])
             if s + 4 < 2 * NCH:
                 x_half((s + 4) // 2, s % 2, psX)
             if s == NG - 1:
@@ -317,14 +344,19 @@ def tile_complexnn_pa_kernel(tc, x, W1, b1, W2, b2, out):
                     slot_t(1, psT)
             if s >= 1:
                 h_max(s - 1)
-            if s % 2 == 0 and (s + 2) // 2 < NCH:
-                x_quant((s + 2) // 2)
+            for t in VE_T:
+                y_op(s, t)
+            if s == 0:
+                x_quant(1, 0)
+            if (s + 3) // 2 < NCH:
+                x_quant((s + 3) // 2, (s + 3) % 2)
             if s == 2:
                 quant_w2(0)
                 quant_w2(1)
+            if s >= 1:
+                h_quant(s - 1)
 
         last = NCH - 1
-        h_quant(NG - 2)
         tail_acc = []
         for fc in range(4):
             acc2 = bank(ps1)

@@ -13,44 +13,39 @@ ALU = mybir.AluOpType
 
 P = 128
 B, D, H, F = 4096, 512, 1024, 512
-CH = 512
-NCH = B // CH
-NJ = H // P
-NG = 2 * NCH
+CHUNK = 512
+HALF = CHUNK // 2
+N_CHUNKS = B // CHUNK
+N_GROUPS = 2 * N_CHUNKS
+N_HIDDEN_TILES = H // P
+N_OUT_TILES = F // P
 FLOPS = 2 * B * D * H + 2 * B * H * F
-
-GP_T = (0, 1, 3)
-VE_T = ()
 
 
 def tile_complexnn_pa_kernel(tc, x, W1, b1, W2, b2, out):
     nc = tc.nc
     with ExitStack() as ctx:
         const = ctx.enter_context(tc.tile_pool(name="const", bufs=1))
-        xin = ctx.enter_context(tc.tile_pool(name="xin", bufs=2 * NCH))
+        xin = ctx.enter_context(tc.tile_pool(name="xin", bufs=2 * N_CHUNKS))
         xq = ctx.enter_context(tc.tile_pool(name="xq", bufs=2))
         act = ctx.enter_context(tc.tile_pool(name="act", bufs=3))
         hgp = ctx.enter_context(tc.tile_pool(name="hgp", bufs=2))
         hcp = ctx.enter_context(tc.tile_pool(name="hcp", bufs=5))
-        yp = ctx.enter_context(tc.tile_pool(name="yp", bufs=3))
-        outp = ctx.enter_context(tc.tile_pool(name="outp", bufs=3))
-        ps1 = ctx.enter_context(tc.psum_pool(name="ps1", bufs=4))
-        psA = ctx.enter_context(tc.psum_pool(name="psA", bufs=2))
-        psT = ctx.enter_context(tc.psum_pool(name="psT", bufs=1))
-        psX = ctx.enter_context(tc.psum_pool(name="psX", bufs=1))
+        yp = ctx.enter_context(tc.tile_pool(name="yp", bufs=4))
+        outp = ctx.enter_context(tc.tile_pool(name="outp", bufs=9))
+        ps_l1 = ctx.enter_context(tc.psum_pool(name="ps_l1", bufs=4))
+        ps_l2 = ctx.enter_context(tc.psum_pool(name="ps_l2", bufs=2))
+        ps_back = ctx.enter_context(tc.psum_pool(name="ps_back", bufs=1))
+        ps_x = ctx.enter_context(tc.psum_pool(name="ps_x", bufs=1))
         ctx.enter_context(tc.manual_schedule())
 
         def bank(pool):
-            if pool is ps1:
-                return ps1.tile([P, 512], F32, name="acc", tag="acc")
-            if pool is psA:
-                return psA.tile([P, 512], F32, name="acc2", tag="acc2")
-            if pool is psT:
-                return psT.tile([P, 512], F32, name="tr", tag="tr")
-            return psX.tile([P, 512], F32, name="xt", tag="xt")
+            return pool.tile([P, 512], F32, name="bank", tag="bank")
 
-        b1_bf = const.tile([P, NJ], BF16)
-        b2_bf = const.tile([P, 4], BF16)
+        warm = const.tile([P, 1], F32)
+        nc.vector.memset(warm[:], 0.0)
+        nc.scalar.activation(out=warm[:], in_=warm[:], func=ACT.Tanh)
+
         x_view = x.rearrange("(c p q) d -> c p (q d)", p=P, q=4)
         x_tiles = {}
 
@@ -59,39 +54,38 @@ def tile_complexnn_pa_kernel(tc, x, W1, b1, W2, b2, out):
             nc.sync.dma_start(out=x_t[:], in_=x_view[c][:, b * 2 * D : (b + 1) * 2 * D])
             x_tiles[(c, b)] = x_t
 
-        w1_raw0 = const.tile([P, 4, 512], BF16)
-        w1_raw1 = const.tile([P, 4, 512], BF16)
-        w2_raw = const.tile([P, NJ, F], BF16)
+        w1_raw = []
 
-        def load_w1(g, dst):
+        def load_w1(g):
+            raw = const.tile([P, 4, 512], BF16, name="w1_raw%d" % g)
             for u in range(2):
                 nc.sync.dma_start(
-                    out=dst[:, 2 * u : 2 * u + 2, :],
+                    out=raw[:, 2 * u : 2 * u + 2, :],
                     in_=W1[256 * u : 256 * u + 256, 512 * g : 512 * g + 512].rearrange(
                         "(q e) c -> q e c", e=2
                     ),
                 )
+            w1_raw.append(raw)
 
+        b1_bf = const.tile([P, N_HIDDEN_TILES], BF16)
+        b2_bf = const.tile([P, N_OUT_TILES], BF16)
         load_x(0, 0)
-        load_w1(0, w1_raw0)
+        load_w1(0)
         load_x(0, 1)
-        with nc.allow_non_contiguous_dma(reason="bias values, one per partition and tile"):
+        with nc.allow_non_contiguous_dma(reason="one bias value for each partition and tile"):
             nc.sync.dma_start(out=b1_bf[:], in_=b1.rearrange("(j m) -> m j", m=P))
             nc.sync.dma_start(out=b2_bf[:], in_=b2.rearrange("(j m) -> m j", m=P))
-        load_w1(1, w1_raw1)
+        load_w1(1)
         load_x(1, 0)
         load_x(1, 1)
+        w2_raw = const.tile([P, N_HIDDEN_TILES, F], BF16)
         nc.sync.dma_start(out=w2_raw[:], in_=W2.rearrange("(j m) f -> m j f", m=P))
-        for c in range(2, NCH):
+        for c in range(2, N_CHUNKS):
             load_x(c, 0)
             load_x(c, 1)
 
         ident = const.tile([P, P], F32)
         make_identity(nc, ident[:])
-
-        b1_f = const.tile([P, NJ], F32)
-        b1_s = const.tile([P, NJ], F32)
-        b2_c = const.tile([P, 4], F32)
 
         w1_g = const.tile([P, H, 4], BF16, align_bytes=64)
         w1_c = const.tile([P, H], U32, align_bytes=64)
@@ -100,29 +94,24 @@ def tile_complexnn_pa_kernel(tc, x, W1, b1, W2, b2, out):
         w2_c = const.tile([P, 2, F], U32, align_bytes=64)
         w2_s = const.tile([P, 2, F], U8, align_bytes=64)
 
-        def regroup_v(dst, src):
-            nc.vector.tensor_copy(
+        def regroup(copy, dst, src):
+            copy(
                 out=dst.rearrange("p (c i) t -> p c t i", i=4),
                 in_=src.rearrange("p t (c i) -> p c t i", i=4),
             )
 
-        def regroup_s(dst, src):
-            nc.scalar.copy(
-                out=dst.rearrange("p (c i) t -> p c t i", i=4),
-                in_=src.rearrange("p t (c i) -> p c t i", i=4),
-            )
-
-        def regroup_g(dst, src):
+        def regroup_on_gpsimd(dst, src):
             nc.gpsimd.tensor_scalar(
                 out=dst, in0=src.rearrange("p t c -> p c t"), scalar1=1.0, scalar2=0.0,
                 op0=ALU.mult, op1=ALU.add,
             )
 
         def quant_w1(c0, c1):
+            cols = slice(c0, c1)
             nc.vector.quantize_mx(
-                out=w1_c[:, c0:c1].bitcast(FP8X4),
-                scales=w1_s[:, c0:c1],
-                in_=w1_g[:, c0:c1, :].rearrange("p c t -> p (c t)"),
+                out=w1_c[:, cols].bitcast(FP8X4),
+                scales=w1_s[:, cols],
+                in_=w1_g[:, cols, :].rearrange("p c t -> p (c t)"),
             )
 
         def quant_w2(g):
@@ -137,51 +126,54 @@ def tile_complexnn_pa_kernel(tc, x, W1, b1, W2, b2, out):
 
         def x_half(c, b, pool):
             if b == 0:
-                xg = xq.tile([P, 4 * CH], BF16, align_bytes=64)
+                xg = xq.tile([P, 4 * CHUNK], BF16, align_bytes=64)
                 xgs[c] = xg
             xw = x_tiles[(c, b)][:].bitcast(F32)
             xt = bank(pool)
             for qq in range(2):
                 for u in range(2):
                     nc.tensor.transpose(
-                        xt[:, u * 256 + qq * P : u * 256 + (qq + 1) * P],
+                        xt[:, u * HALF + qq * P : u * HALF + (qq + 1) * P],
                         xw[:, qq * 256 + u * P : qq * 256 + (u + 1) * P],
                         ident[:],
                     )
             xg_w = xgs[c][:].bitcast(F32).rearrange("p (n u) -> p n u", u=2)
             nc.scalar.copy(
-                out=xg_w[:, b * 256 : (b + 1) * 256, :],
+                out=xg_w[:, b * HALF : (b + 1) * HALF, :],
                 in_=xt[:].rearrange("p (u n) -> p n u", u=2),
             )
 
         def x_quant(c, b):
             if b == 0:
-                xc = xq.tile([P, CH], U32, align_bytes=64)
-                xs = xq.tile([P, CH], U8, align_bytes=64)
+                xc = xq.tile([P, CHUNK], U32, align_bytes=64)
+                xs = xq.tile([P, CHUNK], U8, align_bytes=64)
                 x_codes[c] = (xc, xs)
             xc, xs = x_codes[c]
             nc.vector.quantize_mx(
-                out=xc[:, b * 256 : (b + 1) * 256].bitcast(FP8X4),
-                scales=xs[:, b * 256 : (b + 1) * 256],
-                in_=xgs[c][:, b * 1024 : (b + 1) * 1024],
+                out=xc[:, b * HALF : (b + 1) * HALF].bitcast(FP8X4),
+                scales=xs[:, b * HALF : (b + 1) * HALF],
+                in_=xgs[c][:, b * 4 * HALF : (b + 1) * 4 * HALF],
             )
 
-        tts = {}
-        wts = {}
+        b1_f = const.tile([P, N_HIDDEN_TILES], F32)
+        b1_s = const.tile([P, N_HIDDEN_TILES], F32)
+        b2_f = const.tile([P, N_OUT_TILES], F32)
+        tanhs = {}
+        lins = {}
         accs = {}
         hgs = {}
         h_codes = {}
 
-        def l1_tanh(s, t):
-            xc, xs = x_codes[s // 2]
-            j = 4 * (s % 2) + t
+        def l1_tanh(k, t):
+            xc, xs = x_codes[k // 2]
+            j = 4 * (k % 2) + t
             if t == 0:
-                tt = act.tile([P, 4, CH], F32)
-                wt = act.tile([P, 4, CH], F32)
-                tts[s] = tt
-                wts[s] = wt
-            acc = bank(ps1)
-            accs[(s, t)] = acc
+                tanh_t = act.tile([P, 4, CHUNK], F32)
+                lin_t = act.tile([P, 4, CHUNK], F32)
+                tanhs[k] = tanh_t
+                lins[k] = lin_t
+            acc = bank(ps_l1)
+            accs[(k, t)] = acc
             nc.tensor.matmul_mx(
                 out=acc[:],
                 lhsT=w1_c[:, j * P : (j + 1) * P].bitcast(FP8X4),
@@ -192,186 +184,158 @@ def tile_complexnn_pa_kernel(tc, x, W1, b1, W2, b2, out):
                 stop=True,
             )
             nc.scalar.activation(
-                out=tts[s][:, t, :], in_=acc[:], func=ACT.Tanh, bias=b1_f[:, j : j + 1], scale=1.0
+                out=tanhs[k][:, t, :], in_=acc[:], func=ACT.Tanh, bias=b1_f[:, j : j + 1], scale=1.0
             )
 
-        def u_op(s, t):
+        def add_tanh(k, t):
             nc.vector.scalar_tensor_tensor(
-                out=wts[s][:, t, :], in0=tts[s][:, t, :], scalar=1.0 / 9.0, in1=accs[(s, t)][:],
+                out=lins[k][:, t, :], in0=tanhs[k][:, t, :], scalar=1.0 / 9.0, in1=accs[(k, t)][:],
                 op0=ALU.mult, op1=ALU.add,
             )
 
-        def y_op(s, t):
-            j = 4 * (s % 2) + t
-            if t in VE_T:
-                nc.vector.tensor_scalar(
-                    out=wts[s][:, t, :], in0=wts[s][:, t, :], scalar1=1.8, scalar2=b1_s[:, j : j + 1],
-                    op0=ALU.mult, op1=ALU.add,
-                )
-            elif t in GP_T:
-                nc.gpsimd.tensor_scalar(
-                    out=wts[s][:, t, :], in0=wts[s][:, t, :], scalar1=1.8, scalar2=b1_s[:, j : j + 1],
-                    op0=ALU.mult, op1=ALU.add,
-                )
-            else:
+        def affine(k, t):
+            j = 4 * (k % 2) + t
+            if t == 2:
                 nc.scalar.activation(
-                    out=wts[s][:, t, :], in_=wts[s][:, t, :], func=ACT.Identity,
+                    out=lins[k][:, t, :], in_=lins[k][:, t, :], func=ACT.Identity,
                     bias=b1_s[:, j : j + 1], scale=1.8,
                 )
+            else:
+                nc.gpsimd.tensor_scalar(
+                    out=lins[k][:, t, :], in0=lins[k][:, t, :], scalar1=1.8, scalar2=b1_s[:, j : j + 1],
+                    op0=ALU.mult, op1=ALU.add,
+                )
 
-        def h_max(s):
-            hg = hgp.tile([P, 4 * CH], BF16, align_bytes=64)
-            hgs[s] = hg
+        def h_max(k):
+            hg = hgp.tile([P, 4 * CHUNK], BF16, align_bytes=64)
+            hgs[k] = hg
             nc.vector.tensor_tensor(
                 out=hg[:].rearrange("p (c i t) -> p c t i", i=4, t=4),
-                in0=wts[s][:].rearrange("p t (c i) -> p c t i", i=4),
-                in1=tts[s][:].rearrange("p t (c i) -> p c t i", i=4),
+                in0=lins[k][:].rearrange("p t (c i) -> p c t i", i=4),
+                in1=tanhs[k][:].rearrange("p t (c i) -> p c t i", i=4),
                 op=ALU.max,
             )
 
-        def h_quant(s):
-            hc = hcp.tile([P, CH], U32, align_bytes=64)
-            hs = hcp.tile([P, CH], U8, align_bytes=64)
-            nc.vector.quantize_mx(out=hc[:].bitcast(FP8X4), scales=hs[:], in_=hgs[s][:])
-            h_codes[s] = (hc, hs)
+        def h_quant(k):
+            hc = hcp.tile([P, CHUNK], U32, align_bytes=64)
+            hs = hcp.tile([P, CHUNK], U8, align_bytes=64)
+            nc.vector.quantize_mx(out=hc[:].bitcast(FP8X4), scales=hs[:], in_=hgs[k][:])
+            h_codes[k] = (hc, hs)
 
         out_view = out.rearrange("(c p q) f -> c p q f", p=P, q=4)
         ys = {}
 
-        def l2_pass(acc2, c, fc, g):
+        def product_pass(acc2, c, fo, g):
             hc, hs = h_codes[2 * c + g]
             nc.tensor.matmul_mx(
                 out=acc2[:],
-                lhsT=w2_c[:, g, fc * P : (fc + 1) * P].bitcast(FP8X4),
-                lhsT_scale=w2_s[:, g, fc * P : (fc + 1) * P],
+                lhsT=w2_c[:, g, fo * P : (fo + 1) * P].bitcast(FP8X4),
+                lhsT_scale=w2_s[:, g, fo * P : (fo + 1) * P],
                 rhs=hc[:].bitcast(FP8X4),
                 rhs_scale=hs[:],
                 start=(g == 0),
                 stop=(g == 1),
             )
 
-        def l2_bias(acc2, c, fc, on_vector):
-            y_t = yp.tile([P, CH], F32)
-            ys[(c, fc)] = y_t
+        def add_bias(acc2, c, fo, on_vector):
+            y_t = yp.tile([P, CHUNK], F32)
+            ys[(c, fo)] = y_t
             if on_vector:
                 nc.vector.tensor_scalar(
-                    out=y_t[:], in0=acc2[:], scalar1=0.5, scalar2=b2_c[:, fc : fc + 1],
+                    out=y_t[:], in0=acc2[:], scalar1=0.5, scalar2=b2_f[:, fo : fo + 1],
                     op0=ALU.mult, op1=ALU.add,
                 )
             else:
                 nc.scalar.activation(
-                    out=y_t[:], in_=acc2[:], func=ACT.Identity, bias=b2_c[:, fc : fc + 1], scale=0.5
+                    out=y_t[:], in_=acc2[:], func=ACT.Identity, bias=b2_f[:, fo : fo + 1], scale=0.5
                 )
 
-        def job_l(c, fc):
-            acc2 = bank(psA)
-            l2_pass(acc2, c, fc, 0)
-            l2_pass(acc2, c, fc, 1)
-            l2_bias(acc2, c, fc, False)
-
-        def job_t(c, fc, pool, on_vector):
-            y_t = ys[(c, fc)]
+        def back(c, fo, pool, on_vector):
             tr = bank(pool)
-            for q in range(4):
-                nc.tensor.transpose(tr[:, q * P : (q + 1) * P], y_t[:, q * P : (q + 1) * P], ident[:])
-            o_t = outp.tile([P, 4, P], F32)
+            for n in range(0, CHUNK, P):
+                nc.tensor.transpose(tr[:, n : n + P], ys[(c, fo)][:, n : n + P], ident[:])
+            o_t = outp.tile([P, CHUNK], F32)
             if on_vector:
-                nc.vector.tensor_scalar_max(
-                    out=o_t[:].rearrange("p q f -> p (q f)"), in0=tr[:], scalar1=0.0
-                )
+                nc.vector.tensor_scalar_max(out=o_t[:], in0=tr[:], scalar1=0.0)
             else:
-                nc.scalar.activation(
-                    out=o_t[:].rearrange("p q f -> p (q f)"), in_=tr[:], func=ACT.Relu
-                )
-            nc.sync.dma_start(out=out_view[c][:, :, fc * P : (fc + 1) * P], in_=o_t[:])
+                nc.scalar.activation(out=o_t[:], in_=tr[:], func=ACT.Relu)
+            nc.sync.dma_start(
+                out=out_view[c][:, :, fo * P : (fo + 1) * P],
+                in_=o_t[:].rearrange("p (q f) -> p q f", f=P),
+            )
 
-        regroup_v(w1_g[:, 0:512, :], w1_raw0[:])
-        regroup_g(w1_g[:, 512:768, :], w1_raw1[:, :, 0:256])
-        regroup_g(w1_g[:, 768:1024, :], w1_raw1[:, :, 256:512])
+        def product_n(n):
+            acc2 = bank(ps_l2)
+            product_pass(acc2, n // N_OUT_TILES, n % N_OUT_TILES, 0)
+            product_pass(acc2, n // N_OUT_TILES, n % N_OUT_TILES, 1)
+            add_bias(acc2, n // N_OUT_TILES, n % N_OUT_TILES, False)
+
+        def back_n(n):
+            back(n // N_OUT_TILES, n % N_OUT_TILES, ps_back, False)
+
+        regroup(nc.vector.tensor_copy, w1_g[:, 0:512, :], w1_raw[0][:])
+        regroup_on_gpsimd(w1_g[:, 512:768, :], w1_raw[1][:, :, 0:256])
+        regroup_on_gpsimd(w1_g[:, 768:1024, :], w1_raw[1][:, :, 256:512])
         quant_w1(0, 512)
-        x_half(0, 0, psX)
-        x_half(0, 1, psT)
+        x_half(0, 0, ps_x)
+        x_half(0, 1, ps_back)
         x_quant(0, 0)
         x_quant(0, 1)
         nc.vector.tensor_copy(out=b1_f[:], in_=b1_bf[:])
         nc.vector.tensor_scalar_mul(out=b1_s[:], in0=b1_bf[:], scalar1=1.8)
-        nc.vector.tensor_copy(out=b2_c[:], in_=b2_bf[:])
+        nc.vector.tensor_copy(out=b2_f[:], in_=b2_bf[:])
         l1_tanh(0, 0)
         l1_tanh(0, 1)
-        x_half(1, 0, psX)
+        x_half(1, 0, ps_x)
         l1_tanh(0, 2)
         l1_tanh(0, 3)
-        x_half(1, 1, psT)
-        quant_w1(512, 768)
+        x_half(1, 1, ps_back)
 
-        done = [0, 0]
-        n_main = 4 * (NCH - 1)
-
-        def slot_l(s):
-            n = done[0]
-            if n < n_main and s >= 2 * (n // 4) + 3:
-                job_l(n // 4, n % 4)
-                done[0] = n + 1
-
-        def slot_t(keep, pool):
-            n = done[1]
-            if n < done[0] - keep:
-                job_t(n // 4, n % 4, pool, False)
-                done[1] = n + 1
-
-        for s in range(NG):
+        for s in range(N_GROUPS):
+            n_first = 2 * (s - 3)
             for t in range(4):
-                u_op(s, t)
-                if s == 0 and t == 1:
-                    quant_w1(768, 1024)
-                if s + 1 < NG:
+                add_tanh(s, t)
+                if s == 0 and t % 2 == 0:
+                    quant_w1(512 + 128 * t, 768 + 128 * t)
+                if s + 1 < N_GROUPS:
                     l1_tanh(s + 1, t)
-                if t not in VE_T:
-                    y_op(s, t)
-                if t == 0:
-                    slot_l(s)
-                if t == 1:
-                    slot_t(1, psT)
-            slot_l(s)
-            slot_t(1, psT)
+                affine(s, t)
+                if t == 0 and s >= 3:
+                    product_n(n_first)
+                if t == 1 and s >= 4:
+                    back_n(n_first - 1)
+            if s >= 3:
+                product_n(n_first + 1)
+                back_n(n_first)
             if s < 2:
-                regroup_s(w2_g[:, s, :, :], w2_raw[:, 4 * s : 4 * s + 4, :])
-            if s + 4 < 2 * NCH:
-                x_half((s + 4) // 2, s % 2, psX)
-            if s == NG - 1:
-                for r in range(2):
-                    slot_l(s)
-                    slot_t(1, psT)
+                regroup(nc.scalar.copy, w2_g[:, s, :, :], w2_raw[:, 4 * s : 4 * s + 4, :])
+            if s + 4 < 2 * N_CHUNKS:
+                x_half((s + 4) // 2, s % 2, ps_x)
+            if s == N_GROUPS - 1:
+                for n in range(n_first + 2, n_first + 4):
+                    product_n(n)
+                    back_n(n - 1)
             if s >= 1:
                 h_max(s - 1)
-            for t in VE_T:
-                y_op(s, t)
-            if s == 0:
-                x_quant(1, 0)
-            if (s + 3) // 2 < NCH:
-                x_quant((s + 3) // 2, (s + 3) % 2)
+            for half_chunk in range(2 if s == 0 else s + 3, min(s + 4, 2 * N_CHUNKS)):
+                x_quant(half_chunk // 2, half_chunk % 2)
             if s == 2:
                 quant_w2(0)
                 quant_w2(1)
             if s >= 1:
                 h_quant(s - 1)
 
-        last = NCH - 1
-        tail_acc = []
-        for fc in range(4):
-            acc2 = bank(ps1)
-            tail_acc.append(acc2)
-            l2_pass(acc2, last, fc, 0)
-        spare = [psT, psA, psX, psA]
-        n_spare = n_main - done[1]
-        for r in range(n_spare):
-            slot_t(0, spare[r % 4])
-        h_max(NG - 1)
-        h_quant(NG - 1)
-        for fc in range(4):
-            l2_pass(tail_acc[fc], last, fc, 1)
-            l2_bias(tail_acc[fc], last, fc, fc % 2 == 0)
-            if fc >= 1:
-                job_t(last, fc - 1, spare[n_spare % 4], fc % 2 == 1)
-                n_spare += 1
-        job_t(last, 3, spare[n_spare % 4], False)
+        last = N_CHUNKS - 1
+        last_acc = []
+        for fo in range(N_OUT_TILES):
+            last_acc.append(bank(ps_l1))
+            product_pass(last_acc[fo], last, fo, 0)
+        back_n(N_OUT_TILES * last - 1)
+        h_max(N_GROUPS - 1)
+        h_quant(N_GROUPS - 1)
+        for fo in range(N_OUT_TILES):
+            product_pass(last_acc[fo], last, fo, 1)
+            add_bias(last_acc[fo], last, fo, fo % 2 == 0)
+            if fo >= 1:
+                back(last, fo - 1, ps_l2, fo % 2 == 1)
+        back(last, N_OUT_TILES - 1, ps_l2, False)

@@ -29,19 +29,20 @@ def tile_complexnn_pa_kernel(tc, x, W1, b1, W2, b2, out):
         xin = ctx.enter_context(tc.tile_pool(name="xin", bufs=2 * N_CHUNKS))
         xq = ctx.enter_context(tc.tile_pool(name="xq", bufs=2))
         act = ctx.enter_context(tc.tile_pool(name="act", bufs=3))
+        raw = ctx.enter_context(tc.tile_pool(name="raw", bufs=4))
         hgp = ctx.enter_context(tc.tile_pool(name="hgp", bufs=2))
         hcp = ctx.enter_context(tc.tile_pool(name="hcp", bufs=5))
-        yp = ctx.enter_context(tc.tile_pool(name="yp", bufs=4))
+        yp = ctx.enter_context(tc.tile_pool(name="yp", bufs=6))
         outp = ctx.enter_context(tc.tile_pool(name="outp", bufs=9))
         ps_l1 = ctx.enter_context(tc.psum_pool(name="ps_l1", bufs=4))
-        ps_l2 = ctx.enter_context(tc.psum_pool(name="ps_l2", bufs=2))
-        ps_back = ctx.enter_context(tc.psum_pool(name="ps_back", bufs=1))
-        ps_x = ctx.enter_context(tc.psum_pool(name="ps_x", bufs=1))
+        ps = ctx.enter_context(tc.psum_pool(name="ps", bufs=4))
         ctx.enter_context(tc.manual_schedule())
 
         def bank(pool):
             return pool.tile([P, 512], F32, name="bank", tag="bank")
 
+        b_rows = const.tile([P, P], BF16)
+        nc.vector.memset(b_rows[:], 0.0)
         warm = const.tile([P, 1], F32)
         nc.vector.memset(warm[:], 0.0)
         nc.scalar.activation(out=warm[:], in_=warm[:], func=ACT.Tanh)
@@ -56,26 +57,22 @@ def tile_complexnn_pa_kernel(tc, x, W1, b1, W2, b2, out):
 
         w1_raw = []
 
-        def load_w1(g):
-            raw = const.tile([P, 4, 512], BF16, name="w1_raw%d" % g)
+        def load_w1(c0, c1):
+            raw = const.tile([P, 4, c1 - c0], BF16, name="w1_raw%d" % c0)
             for u in range(2):
                 nc.sync.dma_start(
                     out=raw[:, 2 * u : 2 * u + 2, :],
-                    in_=W1[256 * u : 256 * u + 256, 512 * g : 512 * g + 512].rearrange(
-                        "(q e) c -> q e c", e=2
-                    ),
+                    in_=W1[256 * u : 256 * u + 256, c0:c1].rearrange("(q e) c -> q e c", e=2),
                 )
             w1_raw.append(raw)
 
-        b1_bf = const.tile([P, N_HIDDEN_TILES], BF16)
-        b2_bf = const.tile([P, N_OUT_TILES], BF16)
+        nc.scalar.dma_start(out=b_rows[0:8, :], in_=b1.rearrange("(j m) -> j m", m=P))
+        nc.scalar.dma_start(out=b_rows[8:12, :], in_=b2.rearrange("(j m) -> j m", m=P))
+        load_w1(0, 256)
         load_x(0, 0)
-        load_w1(0)
         load_x(0, 1)
-        with nc.allow_non_contiguous_dma(reason="one bias value for each partition and tile"):
-            nc.sync.dma_start(out=b1_bf[:], in_=b1.rearrange("(j m) -> m j", m=P))
-            nc.sync.dma_start(out=b2_bf[:], in_=b2.rearrange("(j m) -> m j", m=P))
-        load_w1(1)
+        load_w1(256, 512)
+        load_w1(512, 1024)
         load_x(1, 0)
         load_x(1, 1)
         w2_raw = const.tile([P, N_HIDDEN_TILES, F], BF16)
@@ -98,12 +95,6 @@ def tile_complexnn_pa_kernel(tc, x, W1, b1, W2, b2, out):
             copy(
                 out=dst.rearrange("p (c i) t -> p c t i", i=4),
                 in_=src.rearrange("p t (c i) -> p c t i", i=4),
-            )
-
-        def regroup_on_gpsimd(dst, src):
-            nc.gpsimd.tensor_scalar(
-                out=dst, in0=src.rearrange("p t c -> p c t"), scalar1=1.0, scalar2=0.0,
-                op0=ALU.mult, op1=ALU.add,
             )
 
         def quant_w1(c0, c1):
@@ -156,22 +147,28 @@ def tile_complexnn_pa_kernel(tc, x, W1, b1, W2, b2, out):
             )
 
         b1_f = const.tile([P, N_HIDDEN_TILES], F32)
-        b1_s = const.tile([P, N_HIDDEN_TILES], F32)
+        b1_18 = const.tile([P, N_HIDDEN_TILES], F32)
         b2_f = const.tile([P, N_OUT_TILES], F32)
         tanhs = {}
-        lins = {}
+        raws = {}
         accs = {}
         hgs = {}
         h_codes = {}
+        y_slots = const.tile([P, 6, CHUNK], F32)
 
-        def l1_tanh(k, t):
+        def order(k):
+            return (0, 1, 2, 3) if k % 2 == 0 else (2, 3, 0, 1)
+
+        def y_slot(k, t):
+            return y_slots[:, 2 * (k % 2) + t, :]
+
+        def l1_tanh(k, i):
+            t = order(k)[i]
             xc, xs = x_codes[k // 2]
             j = 4 * (k % 2) + t
-            if t == 0:
+            if i == 0:
                 tanh_t = act.tile([P, 4, CHUNK], F32)
-                lin_t = act.tile([P, 4, CHUNK], F32)
                 tanhs[k] = tanh_t
-                lins[k] = lin_t
             acc = bank(ps_l1)
             accs[(k, t)] = acc
             nc.tensor.matmul_mx(
@@ -187,31 +184,32 @@ def tile_complexnn_pa_kernel(tc, x, W1, b1, W2, b2, out):
                 out=tanhs[k][:, t, :], in_=acc[:], func=ACT.Tanh, bias=b1_f[:, j : j + 1], scale=1.0
             )
 
-        def add_tanh(k, t):
+        def add_tanh(k, i):
+            t = order(k)[i]
+            if i < 2:
+                raws[(k, t)] = y_slot(k, t)
+            else:
+                raw_t = raw.tile([P, CHUNK], F32)
+                raws[(k, t)] = raw_t[:]
             nc.vector.scalar_tensor_tensor(
-                out=lins[k][:, t, :], in0=tanhs[k][:, t, :], scalar=1.0 / 9.0, in1=accs[(k, t)][:],
+                out=raws[(k, t)], in0=tanhs[k][:, t, :], scalar=1.0 / 9.0, in1=accs[(k, t)][:],
                 op0=ALU.mult, op1=ALU.add,
             )
 
-        def affine(k, t):
+        def affine(k, i, engine=nc.gpsimd):
+            t = order(k)[i]
             j = 4 * (k % 2) + t
-            if t == 2:
-                nc.scalar.activation(
-                    out=lins[k][:, t, :], in_=lins[k][:, t, :], func=ACT.Identity,
-                    bias=b1_s[:, j : j + 1], scale=1.8,
-                )
-            else:
-                nc.gpsimd.tensor_scalar(
-                    out=lins[k][:, t, :], in0=lins[k][:, t, :], scalar1=1.8, scalar2=b1_s[:, j : j + 1],
-                    op0=ALU.mult, op1=ALU.add,
-                )
+            engine.tensor_scalar(
+                out=y_slot(k, t), in0=raws[(k, t)], scalar1=1.8, scalar2=b1_18[:, j : j + 1],
+                op0=ALU.mult, op1=ALU.add,
+            )
 
         def h_max(k):
             hg = hgp.tile([P, 4 * CHUNK], BF16, align_bytes=64)
             hgs[k] = hg
             nc.vector.tensor_tensor(
                 out=hg[:].rearrange("p (c i t) -> p c t i", i=4, t=4),
-                in0=lins[k][:].rearrange("p t (c i) -> p c t i", i=4),
+                in0=y_slots[:, 2 * (k % 2) : 2 * (k % 2) + 4, :].rearrange("p t (c i) -> p c t i", i=4),
                 in1=tanhs[k][:].rearrange("p t (c i) -> p c t i", i=4),
                 op=ALU.max,
             )
@@ -265,77 +263,88 @@ def tile_complexnn_pa_kernel(tc, x, W1, b1, W2, b2, out):
             )
 
         def product_n(n):
-            acc2 = bank(ps_l2)
+            acc2 = bank(ps)
             product_pass(acc2, n // N_OUT_TILES, n % N_OUT_TILES, 0)
             product_pass(acc2, n // N_OUT_TILES, n % N_OUT_TILES, 1)
             add_bias(acc2, n // N_OUT_TILES, n % N_OUT_TILES, False)
 
         def back_n(n):
-            back(n // N_OUT_TILES, n % N_OUT_TILES, ps_back, False)
+            back(n // N_OUT_TILES, n % N_OUT_TILES, ps, False)
 
-        regroup(nc.vector.tensor_copy, w1_g[:, 0:512, :], w1_raw[0][:])
-        regroup_on_gpsimd(w1_g[:, 512:768, :], w1_raw[1][:, :, 0:256])
-        regroup_on_gpsimd(w1_g[:, 768:1024, :], w1_raw[1][:, :, 256:512])
-        quant_w1(0, 512)
-        x_half(0, 0, ps_x)
-        x_half(0, 1, ps_back)
+        b_rows_f = const.tile([P, P], F32)
+        nc.vector.tensor_copy(out=b_rows_f[:], in_=b_rows[:])
+        regroup(nc.vector.tensor_copy, w1_g[:, 0:256, :], w1_raw[0][:])
+        b_cols = bank(ps)
+        nc.tensor.transpose(b_cols[:, 0:P], b_rows_f[:], ident[:])
+        nc.vector.tensor_copy(out=b1_f[:], in_=b_cols[:, 0:8])
+        nc.vector.tensor_scalar_mul(out=b1_18[:], in0=b_cols[:, 0:8], scalar1=1.8)
+        nc.vector.tensor_copy(out=b2_f[:], in_=b_cols[:, 8:12])
+        quant_w1(0, 256)
+        x_half(0, 0, ps)
+        x_half(0, 1, ps)
         x_quant(0, 0)
+        regroup(nc.vector.tensor_copy, w1_g[:, 256:512, :], w1_raw[1][:])
         x_quant(0, 1)
-        nc.vector.tensor_copy(out=b1_f[:], in_=b1_bf[:])
-        nc.vector.tensor_scalar_mul(out=b1_s[:], in0=b1_bf[:], scalar1=1.8)
-        nc.vector.tensor_copy(out=b2_f[:], in_=b2_bf[:])
+        quant_w1(256, 512)
+        regroup(nc.scalar.copy, w1_g[:, 512:768, :], w1_raw[2][:, :, 0:256])
+        regroup(nc.vector.tensor_copy, w1_g[:, 768:1024, :], w1_raw[2][:, :, 256:512])
         l1_tanh(0, 0)
         l1_tanh(0, 1)
-        x_half(1, 0, ps_x)
+        quant_w1(512, 1024)
         l1_tanh(0, 2)
         l1_tanh(0, 3)
-        x_half(1, 1, ps_back)
+        x_half(1, 0, ps)
+        x_half(1, 1, ps)
+
+        def products_until(s):
+            return 4 * (N_CHUNKS - 1) if s == N_GROUPS - 1 else max(0, 2 * (s - 2))
 
         for s in range(N_GROUPS):
-            n_first = 2 * (s - 3)
-            for t in range(4):
-                add_tanh(s, t)
-                if s == 0 and t % 2 == 0:
-                    quant_w1(512 + 128 * t, 768 + 128 * t)
+            if s >= 1:
+                affine(s - 1, 2)
+                affine(s - 1, 3)
+            for i in range(4):
+                add_tanh(s, i)
                 if s + 1 < N_GROUPS:
-                    l1_tanh(s + 1, t)
-                affine(s, t)
-                if t == 0 and s >= 3:
-                    product_n(n_first)
-                if t == 1 and s >= 4:
-                    back_n(n_first - 1)
-            if s >= 3:
-                product_n(n_first + 1)
-                back_n(n_first)
-            if s < 2:
-                regroup(nc.scalar.copy, w2_g[:, s, :, :], w2_raw[:, 4 * s : 4 * s + 4, :])
-            if s + 4 < 2 * N_CHUNKS:
-                x_half((s + 4) // 2, s % 2, ps_x)
-            if s == N_GROUPS - 1:
-                for n in range(n_first + 2, n_first + 4):
-                    product_n(n)
-                    back_n(n - 1)
+                    l1_tanh(s + 1, i)
+                if i < 2:
+                    affine(s, i)
+            if s == 3:
+                quant_w2(1)
+            if s >= 2:
+                h_quant(s - 2)
             if s >= 1:
                 h_max(s - 1)
+            for n in range(products_until(s - 1), products_until(s)):
+                product_n(n)
+            backs = list(range(products_until(s - 2), products_until(s - 1)))
+            for n in backs[:1]:
+                back_n(n)
+            if s in (1, 2):
+                regroup(nc.scalar.copy, w2_g[:, s - 1, :, :], w2_raw[:, 4 * s - 4 : 4 * s, :])
+            if s + 4 < 2 * N_CHUNKS:
+                x_half((s + 4) // 2, s % 2, ps)
+            for n in backs[1:]:
+                back_n(n)
             for half_chunk in range(2 if s == 0 else s + 3, min(s + 4, 2 * N_CHUNKS)):
                 x_quant(half_chunk // 2, half_chunk % 2)
             if s == 2:
                 quant_w2(0)
-                quant_w2(1)
-            if s >= 1:
-                h_quant(s - 1)
 
         last = N_CHUNKS - 1
+        for n in range(products_until(N_GROUPS - 2), products_until(N_GROUPS - 1)):
+            back_n(n)
+        affine(N_GROUPS - 1, 2, nc.vector)
+        affine(N_GROUPS - 1, 3, nc.vector)
+        h_quant(N_GROUPS - 2)
+        h_max(N_GROUPS - 1)
         last_acc = []
         for fo in range(N_OUT_TILES):
             last_acc.append(bank(ps_l1))
             product_pass(last_acc[fo], last, fo, 0)
-        back_n(N_OUT_TILES * last - 1)
-        h_max(N_GROUPS - 1)
         h_quant(N_GROUPS - 1)
         for fo in range(N_OUT_TILES):
             product_pass(last_acc[fo], last, fo, 1)
             add_bias(last_acc[fo], last, fo, fo % 2 == 0)
-            if fo >= 1:
-                back(last, fo - 1, ps_l2, fo % 2 == 1)
-        back(last, N_OUT_TILES - 1, ps_l2, False)
+        for fo in range(N_OUT_TILES):
+            back(last, fo, ps, fo % 2 == 0)

@@ -29,7 +29,7 @@ def tile_complexnn_pa_kernel(tc, x, W1, b1, W2, b2, out):
         xin = ctx.enter_context(tc.tile_pool(name="xin", bufs=2 * N_CHUNKS))
         xq = ctx.enter_context(tc.tile_pool(name="xq", bufs=2))
         act = ctx.enter_context(tc.tile_pool(name="act", bufs=3))
-        raw = ctx.enter_context(tc.tile_pool(name="raw", bufs=4))
+        yh = ctx.enter_context(tc.tile_pool(name="yh", bufs=3))
         hgp = ctx.enter_context(tc.tile_pool(name="hgp", bufs=2))
         hcp = ctx.enter_context(tc.tile_pool(name="hcp", bufs=5))
         yp = ctx.enter_context(tc.tile_pool(name="yp", bufs=6))
@@ -150,20 +150,13 @@ def tile_complexnn_pa_kernel(tc, x, W1, b1, W2, b2, out):
         b1_18 = const.tile([P, N_HIDDEN_TILES], F32)
         b2_f = const.tile([P, N_OUT_TILES], F32)
         tanhs = {}
-        raws = {}
         accs = {}
         hgs = {}
         h_codes = {}
-        y_slots = const.tile([P, 6, CHUNK], F32)
-
-        def order(k):
-            return (0, 1, 2, 3) if k % 2 == 0 else (2, 3, 0, 1)
-
-        def y_slot(k, t):
-            return y_slots[:, 2 * (k % 2) + t, :]
+        ys_h = {}
 
         def l1_tanh(k, i):
-            t = order(k)[i]
+            t = i
             xc, xs = x_codes[k // 2]
             j = 4 * (k % 2) + t
             if i == 0:
@@ -184,32 +177,34 @@ def tile_complexnn_pa_kernel(tc, x, W1, b1, W2, b2, out):
                 out=tanhs[k][:, t, :], in_=acc[:], func=ACT.Tanh, bias=b1_f[:, j : j + 1], scale=1.0
             )
 
-        def add_tanh(k, i):
-            t = order(k)[i]
-            if i < 2:
-                raws[(k, t)] = y_slot(k, t)
-            else:
-                raw_t = raw.tile([P, CHUNK], F32)
-                raws[(k, t)] = raw_t[:]
+        def add_tanh(k, t):
+            if t == 0:
+                y_t = yh.tile([P, 4, CHUNK], F32)
+                ys_h[k] = y_t
             nc.vector.scalar_tensor_tensor(
-                out=raws[(k, t)], in0=tanhs[k][:, t, :], scalar=1.0 / 9.0, in1=accs[(k, t)][:],
+                out=ys_h[k][:, t, :], in0=tanhs[k][:, t, :], scalar=1.0 / 9.0, in1=accs[(k, t)][:],
                 op0=ALU.mult, op1=ALU.add,
             )
 
-        def affine(k, i, engine=nc.gpsimd):
-            t = order(k)[i]
+        def affine(k, t):
             j = 4 * (k % 2) + t
-            engine.tensor_scalar(
-                out=y_slot(k, t), in0=raws[(k, t)], scalar1=1.8, scalar2=b1_18[:, j : j + 1],
-                op0=ALU.mult, op1=ALU.add,
-            )
+            y = ys_h[k][:, t, :]
+            if affine_engine(k, t) == "S":
+                nc.scalar.activation(out=y, in_=y, func=ACT.Identity, bias=b1_18[:, j : j + 1], scale=1.8)
+            else:
+                (nc.gpsimd if affine_engine(k, t) == "G" else nc.vector).tensor_scalar(
+                    out=y, in0=y, scalar1=1.8, scalar2=b1_18[:, j : j + 1], op0=ALU.mult, op1=ALU.add
+                )
+
+        def affine_engine(k, t):
+            return "GGGS"[t]
 
         def h_max(k):
             hg = hgp.tile([P, 4 * CHUNK], BF16, align_bytes=64)
             hgs[k] = hg
             nc.vector.tensor_tensor(
                 out=hg[:].rearrange("p (c i t) -> p c t i", i=4, t=4),
-                in0=y_slots[:, 2 * (k % 2) : 2 * (k % 2) + 4, :].rearrange("p t (c i) -> p c t i", i=4),
+                in0=ys_h[k][:].rearrange("p t (c i) -> p c t i", i=4),
                 in1=tanhs[k][:].rearrange("p t (c i) -> p c t i", i=4),
                 op=ALU.max,
             )
@@ -276,9 +271,9 @@ def tile_complexnn_pa_kernel(tc, x, W1, b1, W2, b2, out):
         regroup(nc.vector.tensor_copy, w1_g[:, 0:256, :], w1_raw[0][:])
         b_cols = bank(ps)
         nc.tensor.transpose(b_cols[:, 0:P], b_rows_f[:], ident[:])
-        nc.vector.tensor_copy(out=b1_f[:], in_=b_cols[:, 0:8])
-        nc.vector.tensor_scalar_mul(out=b1_18[:], in0=b_cols[:, 0:8], scalar1=1.8)
-        nc.vector.tensor_copy(out=b2_f[:], in_=b_cols[:, 8:12])
+        nc.scalar.copy(out=b1_f[:], in_=b_cols[:, 0:8])
+        nc.scalar.mul(out=b1_18[:], in_=b_cols[:, 0:8], mul=1.8)
+        nc.scalar.copy(out=b2_f[:], in_=b_cols[:, 8:12])
         quant_w1(0, 256)
         x_half(0, 0, ps)
         x_half(0, 1, ps)
@@ -297,20 +292,22 @@ def tile_complexnn_pa_kernel(tc, x, W1, b1, W2, b2, out):
         x_half(1, 1, ps)
 
         def products_until(s):
-            return 4 * (N_CHUNKS - 1) if s == N_GROUPS - 1 else max(0, 2 * (s - 2))
+            return 4 * (N_CHUNKS - 1) if s == N_GROUPS - 1 else max(0, 2 * (s - 3))
 
         for s in range(N_GROUPS):
-            if s >= 1:
-                affine(s - 1, 2)
-                affine(s - 1, 3)
-            for i in range(4):
-                add_tanh(s, i)
+            for t in range(4):
+                add_tanh(s, t)
                 if s + 1 < N_GROUPS:
-                    l1_tanh(s + 1, i)
-                if i < 2:
-                    affine(s, i)
-            if s == 3:
-                quant_w2(1)
+                    l1_tanh(s + 1, t)
+                if affine_engine(s, t) == "G":
+                    affine(s, t)
+            for t in range(4):
+                if s >= 1 and affine_engine(s - 1, t) == "V":
+                    affine(s - 1, t)
+                if affine_engine(s, t) == "S":
+                    affine(s, t)
+            if s in (3, 4):
+                quant_w2(s - 3)
             if s >= 2:
                 h_quant(s - 2)
             if s >= 1:
@@ -320,22 +317,21 @@ def tile_complexnn_pa_kernel(tc, x, W1, b1, W2, b2, out):
             backs = list(range(products_until(s - 2), products_until(s - 1)))
             for n in backs[:1]:
                 back_n(n)
-            if s in (1, 2):
-                regroup(nc.scalar.copy, w2_g[:, s - 1, :, :], w2_raw[:, 4 * s - 4 : 4 * s, :])
+            if s in (2, 3):
+                regroup(nc.scalar.copy, w2_g[:, s - 2, :, :], w2_raw[:, 4 * s - 8 : 4 * s - 4, :])
             if s + 4 < 2 * N_CHUNKS:
                 x_half((s + 4) // 2, s % 2, ps)
             for n in backs[1:]:
                 back_n(n)
             for half_chunk in range(2 if s == 0 else s + 3, min(s + 4, 2 * N_CHUNKS)):
                 x_quant(half_chunk // 2, half_chunk % 2)
-            if s == 2:
-                quant_w2(0)
 
         last = N_CHUNKS - 1
         for n in range(products_until(N_GROUPS - 2), products_until(N_GROUPS - 1)):
             back_n(n)
-        affine(N_GROUPS - 1, 2, nc.vector)
-        affine(N_GROUPS - 1, 3, nc.vector)
+        for t in range(4):
+            if affine_engine(N_GROUPS - 1, t) == "V":
+                affine(N_GROUPS - 1, t)
         h_quant(N_GROUPS - 2)
         h_max(N_GROUPS - 1)
         last_acc = []

@@ -27,7 +27,7 @@ def tile_complexnn_pa_kernel(tc, x, W1, b1, W2, b2, out):
     with ExitStack() as ctx:
         const = ctx.enter_context(tc.tile_pool(name="const", bufs=1))
         xin = ctx.enter_context(tc.tile_pool(name="xin", bufs=2 * N_CHUNKS))
-        xq = ctx.enter_context(tc.tile_pool(name="xq", bufs=2))
+        xq = ctx.enter_context(tc.tile_pool(name="xq", bufs=6))
         act = ctx.enter_context(tc.tile_pool(name="act", bufs=3))
         yh = ctx.enter_context(tc.tile_pool(name="yh", bufs=3))
         hgp = ctx.enter_context(tc.tile_pool(name="hgp", bufs=2))
@@ -45,7 +45,6 @@ def tile_complexnn_pa_kernel(tc, x, W1, b1, W2, b2, out):
         nc.vector.memset(b_rows[:], 0.0)
         warm = const.tile([P, 1], F32)
         nc.vector.memset(warm[:], 0.0)
-        nc.scalar.activation(out=warm[:], in_=warm[:], func=ACT.Tanh)
 
         x_view = x.rearrange("(c p q) d -> c p (q d)", p=P, q=4)
         x_tiles = {}
@@ -68,6 +67,7 @@ def tile_complexnn_pa_kernel(tc, x, W1, b1, W2, b2, out):
 
         nc.scalar.dma_start(out=b_rows[0:8, :], in_=b1.rearrange("(j m) -> j m", m=P))
         nc.scalar.dma_start(out=b_rows[8:12, :], in_=b2.rearrange("(j m) -> j m", m=P))
+        nc.scalar.activation(out=warm[:], in_=warm[:], func=ACT.Tanh)
         load_w1(0, 256)
         load_x(0, 0)
         load_x(0, 1)
@@ -76,8 +76,9 @@ def tile_complexnn_pa_kernel(tc, x, W1, b1, W2, b2, out):
         load_x(1, 0)
         load_x(1, 1)
         w2_raw = const.tile([P, N_HIDDEN_TILES, F], BF16)
-        nc.sync.dma_start(out=w2_raw[:], in_=W2.rearrange("(j m) f -> m j f", m=P))
         for c in range(2, N_CHUNKS):
+            if c == 4:
+                nc.sync.dma_start(out=w2_raw[:], in_=W2.rearrange("(j m) f -> m j f", m=P))
             load_x(c, 0)
             load_x(c, 1)
 
@@ -197,7 +198,7 @@ def tile_complexnn_pa_kernel(tc, x, W1, b1, W2, b2, out):
                 )
 
         def affine_engine(k, t):
-            return "GGGS"[t]
+            return ("GGGS" if k < 12 else "GGSS")[t]
 
         def h_max(k):
             hg = hgp.tile([P, 4 * CHUNK], BF16, align_bytes=64)
@@ -244,9 +245,19 @@ def tile_complexnn_pa_kernel(tc, x, W1, b1, W2, b2, out):
                 )
 
         def back(c, fo, pool, on_vector):
+            turn(c, fo, pool)
+            leave(c, fo, on_vector)
+
+        turned = {}
+
+        def turn(c, fo, pool):
             tr = bank(pool)
+            turned[(c, fo)] = tr
             for n in range(0, CHUNK, P):
                 nc.tensor.transpose(tr[:, n : n + P], ys[(c, fo)][:, n : n + P], ident[:])
+
+        def leave(c, fo, on_vector):
+            tr = turned[(c, fo)]
             o_t = outp.tile([P, CHUNK], F32)
             if on_vector:
                 nc.vector.tensor_scalar_max(out=o_t[:], in0=tr[:], scalar1=0.0)
@@ -264,22 +275,24 @@ def tile_complexnn_pa_kernel(tc, x, W1, b1, W2, b2, out):
             add_bias(acc2, n // N_OUT_TILES, n % N_OUT_TILES, False)
 
         def back_n(n):
-            back(n // N_OUT_TILES, n % N_OUT_TILES, ps, False)
+            turn(n // N_OUT_TILES, n % N_OUT_TILES, ps)
+            if n not in (16, 18):
+                leave(n // N_OUT_TILES, n % N_OUT_TILES, False)
 
-        b_rows_f = const.tile([P, P], F32)
-        nc.vector.tensor_copy(out=b_rows_f[:], in_=b_rows[:])
         regroup(nc.vector.tensor_copy, w1_g[:, 0:256, :], w1_raw[0][:])
-        b_cols = bank(ps)
-        nc.tensor.transpose(b_cols[:, 0:P], b_rows_f[:], ident[:])
-        nc.scalar.copy(out=b1_f[:], in_=b_cols[:, 0:8])
-        nc.scalar.mul(out=b1_18[:], in_=b_cols[:, 0:8], mul=1.8)
-        nc.scalar.copy(out=b2_f[:], in_=b_cols[:, 8:12])
-        quant_w1(0, 256)
         x_half(0, 0, ps)
         x_half(0, 1, ps)
+        quant_w1(0, 256)
+        b_rows_f = const.tile([P, P], F32)
+        nc.vector.tensor_copy(out=b_rows_f[:], in_=b_rows[:])
+        b_cols = bank(ps)
+        nc.tensor.transpose(b_cols[:, 0:P], b_rows_f[:], ident[:])
         x_quant(0, 0)
         regroup(nc.vector.tensor_copy, w1_g[:, 256:512, :], w1_raw[1][:])
         x_quant(0, 1)
+        nc.vector.tensor_copy(out=b1_f[:], in_=b_cols[:, 0:8])
+        nc.vector.tensor_scalar_mul(out=b1_18[:], in0=b_cols[:, 0:8], scalar1=1.8)
+        nc.vector.tensor_copy(out=b2_f[:], in_=b_cols[:, 8:12])
         quant_w1(256, 512)
         regroup(nc.scalar.copy, w1_g[:, 512:768, :], w1_raw[2][:, :, 0:256])
         regroup(nc.vector.tensor_copy, w1_g[:, 768:1024, :], w1_raw[2][:, :, 256:512])
@@ -292,8 +305,9 @@ def tile_complexnn_pa_kernel(tc, x, W1, b1, W2, b2, out):
         x_half(1, 1, ps)
 
         def products_until(s):
-            return 4 * (N_CHUNKS - 1) if s == N_GROUPS - 1 else max(0, 2 * (s - 3))
+            return 4 * (N_CHUNKS - 1) if s == N_GROUPS - 1 else max(0, 2 * (s - 2))
 
+        x_plan = {0: (4, 5, 6), 1: (7,), 2: (8,), 3: (9, 10, 11, 12), 4: (13,), 5: (14,), 6: (15,)}
         for s in range(N_GROUPS):
             for t in range(4):
                 add_tanh(s, t)
@@ -306,41 +320,49 @@ def tile_complexnn_pa_kernel(tc, x, W1, b1, W2, b2, out):
                     affine(s - 1, t)
                 if affine_engine(s, t) == "S":
                     affine(s, t)
-            if s in (3, 4):
-                quant_w2(s - 3)
-            if s >= 2:
-                h_quant(s - 2)
             if s >= 1:
                 h_max(s - 1)
+            for half_chunk in range(2 if s == 0 else s + 3, min(s + 4, 2 * N_CHUNKS)):
+                x_quant(half_chunk // 2, half_chunk % 2)
+            if s == 3:
+                quant_w2(0)
+                quant_w2(1)
+            if s in (13, 14):
+                n = products_until(s - 3)
+                leave(n // N_OUT_TILES, n % N_OUT_TILES, True)
+            if s >= 1:
+                h_quant(s - 1)
             for n in range(products_until(s - 1), products_until(s)):
                 product_n(n)
             backs = list(range(products_until(s - 2), products_until(s - 1)))
             for n in backs[:1]:
                 back_n(n)
-            if s in (2, 3):
-                regroup(nc.scalar.copy, w2_g[:, s - 2, :, :], w2_raw[:, 4 * s - 8 : 4 * s - 4, :])
-            if s + 4 < 2 * N_CHUNKS:
-                x_half((s + 4) // 2, s % 2, ps)
+            if s in (1, 2):
+                regroup(nc.scalar.copy, w2_g[:, s - 1, :, :], w2_raw[:, 4 * s - 4 : 4 * s, :])
             for n in backs[1:]:
                 back_n(n)
-            for half_chunk in range(2 if s == 0 else s + 3, min(s + 4, 2 * N_CHUNKS)):
-                x_quant(half_chunk // 2, half_chunk % 2)
+            for half_chunk in x_plan.get(s, ()):
+                x_half(half_chunk // 2, half_chunk % 2, ps)
 
         last = N_CHUNKS - 1
-        for n in range(products_until(N_GROUPS - 2), products_until(N_GROUPS - 1)):
-            back_n(n)
         for t in range(4):
             if affine_engine(N_GROUPS - 1, t) == "V":
                 affine(N_GROUPS - 1, t)
-        h_quant(N_GROUPS - 2)
         h_max(N_GROUPS - 1)
+        h_quant(N_GROUPS - 1)
+        backs = list(range(products_until(N_GROUPS - 2), products_until(N_GROUPS - 1)))
+        for n in backs[:1]:
+            back_n(n)
         last_acc = []
         for fo in range(N_OUT_TILES):
             last_acc.append(bank(ps_l1))
             product_pass(last_acc[fo], last, fo, 0)
-        h_quant(N_GROUPS - 1)
+        for n in backs[1:4]:
+            back_n(n)
         for fo in range(N_OUT_TILES):
             product_pass(last_acc[fo], last, fo, 1)
             add_bias(last_acc[fo], last, fo, fo % 2 == 0)
+        for n in backs[4:]:
+            back_n(n)
         for fo in range(N_OUT_TILES):
             back(last, fo, ps, fo % 2 == 0)

@@ -204,9 +204,9 @@ def tile_complexnn_pa_kernel(tc, x, W1, b1, W2, b2, out):
             hg = hgp.tile([P, 4 * CHUNK], BF16, align_bytes=64)
             hgs[k] = hg
             nc.vector.tensor_tensor(
-                out=hg[:].rearrange("p (c i t) -> p c t i", i=4, t=4),
-                in0=ys_h[k][:].rearrange("p t (c i) -> p c t i", i=4),
-                in1=tanhs[k][:].rearrange("p t (c i) -> p c t i", i=4),
+                out=hg[:].rearrange("p (c i t) -> p c t i", i=8, t=4),
+                in0=ys_h[k][:].rearrange("p t (c i) -> p c t i", i=8),
+                in1=tanhs[k][:].rearrange("p t (c i) -> p c t i", i=8),
                 op=ALU.max,
             )
 

@@ -198,7 +198,7 @@ def tile_complexnn_pa_kernel(tc, x, W1, b1, W2, b2, out):
                 )
 
         def affine_engine(k, t):
-            return ("GGGS" if k < 12 else "GGSS")[t]
+            return ("GGGS" if k < 13 else "GGSS")[t]
 
         def h_max(k):
             hg = hgp.tile([P, 4 * CHUNK], BF16, align_bytes=64)
@@ -307,7 +307,6 @@ def tile_complexnn_pa_kernel(tc, x, W1, b1, W2, b2, out):
         def products_until(s):
             return 4 * (N_CHUNKS - 1) if s == N_GROUPS - 1 else max(0, 2 * (s - 2))
 
-        x_plan = {0: (4, 5, 6), 1: (7,), 2: (8,), 3: (9, 10, 11, 12), 4: (13,), 5: (14,), 6: (15,)}
         for s in range(N_GROUPS):
             for t in range(4):
                 add_tanh(s, t)
@@ -341,7 +340,7 @@ def tile_complexnn_pa_kernel(tc, x, W1, b1, W2, b2, out):
                 regroup(nc.scalar.copy, w2_g[:, s - 1, :, :], w2_raw[:, 4 * s - 4 : 4 * s, :])
             for n in backs[1:]:
                 back_n(n)
-            for half_chunk in x_plan.get(s, ()):
+            for half_chunk in range(4 if s == 0 else s + 6, min(s + 7, 2 * N_CHUNKS)):
                 x_half(half_chunk // 2, half_chunk % 2, ps)
 
         last = N_CHUNKS - 1

from contextlib import ExitStack

import concourse.mybir as mybir
from concourse.masks import make_identity

F32 = mybir.dt.float32
BF16 = mybir.dt.bfloat16
U32 = mybir.dt.uint32
U8 = mybir.dt.uint8
FP8X4 = mybir.dt.float8_e4m3fn_x4
ACT = mybir.ActivationFunctionType
ALU = mybir.AluOpType

P = 128
B, D, H, F = 4096, 512, 1024, 512
CHUNK = 512
HALF = CHUNK // 2
N_CHUNKS = B // CHUNK
N_GROUPS = 2 * N_CHUNKS
N_HIDDEN_TILES = H // P
N_OUT_TILES = F // P
FLOPS = 2 * B * D * H + 2 * B * H * F


def tile_complexnn_pa_kernel(tc, x, W1, b1, W2, b2, out):
    nc = tc.nc
    with ExitStack() as ctx:
        const = ctx.enter_context(tc.tile_pool(name="const", bufs=1))
        xin = ctx.enter_context(tc.tile_pool(name="xin", bufs=2 * N_CHUNKS))
        xq = ctx.enter_context(tc.tile_pool(name="xq", bufs=6))
        act = ctx.enter_context(tc.tile_pool(name="act", bufs=3))
        yh = ctx.enter_context(tc.tile_pool(name="yh", bufs=3))
        hgp = ctx.enter_context(tc.tile_pool(name="hgp", bufs=2))
        hcp = ctx.enter_context(tc.tile_pool(name="hcp", bufs=5))
        yp = ctx.enter_context(tc.tile_pool(name="yp", bufs=6))
        outp = ctx.enter_context(tc.tile_pool(name="outp", bufs=9))
        ps_l1 = ctx.enter_context(tc.psum_pool(name="ps_l1", bufs=4))
        ps = ctx.enter_context(tc.psum_pool(name="ps", bufs=4))
        ctx.enter_context(tc.manual_schedule())

        def bank(pool):
            return pool.tile([P, 512], F32, name="bank", tag="bank")

        b_rows = const.tile([P, P], BF16)
        nc.vector.memset(b_rows[:], 0.0)
        warm = const.tile([P, 1], F32)
        nc.vector.memset(warm[:], 0.0)

        x_view = x.rearrange("(c p q) d -> c p (q d)", p=P, q=4)
        x_tiles = {}

        def load_x(c, b):
            x_t = xin.tile([P, 2 * D], BF16)
            nc.sync.dma_start(out=x_t[:], in_=x_view[c][:, b * 2 * D : (b + 1) * 2 * D])
            x_tiles[(c, b)] = x_t

        w1_raw = []

        def load_w1(c0, c1):
            raw = const.tile([P, 4, c1 - c0], BF16, name="w1_raw%d" % c0)
            for u in range(2):
                nc.sync.dma_start(
                    out=raw[:, 2 * u : 2 * u + 2, :],
                    in_=W1[256 * u : 256 * u + 256, c0:c1].rearrange("(q e) c -> q e c", e=2),
                )
            w1_raw.append(raw)

        nc.scalar.dma_start(out=b_rows[0:8, :], in_=b1.rearrange("(j m) -> j m", m=P))
        nc.scalar.dma_start(out=b_rows[8:12, :], in_=b2.rearrange("(j m) -> j m", m=P))
        nc.scalar.activation(out=warm[:], in_=warm[:], func=ACT.Tanh)
        load_w1(0, 256)
        load_x(0, 0)
        load_x(0, 1)
        load_w1(256, 512)
        load_w1(512, 1024)
        load_x(1, 0)
        load_x(1, 1)
        w2_raw = const.tile([P, N_HIDDEN_TILES, F], BF16)
        for c in range(2, N_CHUNKS):
            if c == 4:
                nc.sync.dma_start(out=w2_raw[:], in_=W2.rearrange("(j m) f -> m j f", m=P))
            load_x(c, 0)
            load_x(c, 1)

        ident = const.tile([P, P], F32)
        make_identity(nc, ident[:])

        w1_g = const.tile([P, H, 4], BF16, align_bytes=64)
        w1_c = const.tile([P, H], U32, align_bytes=64)
        w1_s = const.tile([P, H], U8, align_bytes=64)
        w2_g = const.tile([P, 2, F, 4], BF16, align_bytes=64)
        w2_c = const.tile([P, 2, F], U32, align_bytes=64)
        w2_s = const.tile([P, 2, F], U8, align_bytes=64)

        def regroup(copy, dst, src):
            copy(
                out=dst.rearrange("p (c i) t -> p c t i", i=4),
                in_=src.rearrange("p t (c i) -> p c t i", i=4),
            )

        def quant_w1(c0, c1):
            cols = slice(c0, c1)
            nc.vector.quantize_mx(
                out=w1_c[:, cols].bitcast(FP8X4),
                scales=w1_s[:, cols],
                in_=w1_g[:, cols, :].rearrange("p c t -> p (c t)"),
            )

        def quant_w2(g):
            nc.vector.quantize_mx(
                out=w2_c[:, g, :].bitcast(FP8X4),
                scales=w2_s[:, g, :],
                in_=w2_g[:, g, :, :].rearrange("p c t -> p (c t)"),
            )

        xgs = {}
        x_codes = {}

        def x_half(c, b, pool):
            if b == 0:
                xg = xq.tile([P, 4 * CHUNK], BF16, align_bytes=64)
                xgs[c] = xg
            xw = x_tiles[(c, b)][:].bitcast(F32)
            xt = bank(pool)
            for qq in range(2):
                for u in range(2):
                    nc.tensor.transpose(
                        xt[:, u * HALF + qq * P : u * HALF + (qq + 1) * P],
                        xw[:, qq * 256 + u * P : qq * 256 + (u + 1) * P],
                        ident[:],
                    )
            xg_w = xgs[c][:].bitcast(F32).rearrange("p (n u) -> p n u", u=2)
            nc.scalar.copy(
                out=xg_w[:, b * HALF : (b + 1) * HALF, :],
                in_=xt[:].rearrange("p (u n) -> p n u", u=2),
            )

        def x_quant(c, b):
            if b == 0:
                xc = xq.tile([P, CHUNK], U32, align_bytes=64)
                xs = xq.tile([P, CHUNK], U8, align_bytes=64)
                x_codes[c] = (xc, xs)
            xc, xs = x_codes[c]
            nc.vector.quantize_mx(
                out=xc[:, b * HALF : (b + 1) * HALF].bitcast(FP8X4),
                scales=xs[:, b * HALF : (b + 1) * HALF],
                in_=xgs[c][:, b * 4 * HALF : (b + 1) * 4 * HALF],
            )

        b1_f = const.tile([P, N_HIDDEN_TILES], F32)
        b1_18 = const.tile([P, N_HIDDEN_TILES], F32)
        b2_f = const.tile([P, N_OUT_TILES], F32)
        tanhs = {}
        accs = {}
        hgs = {}
        h_codes = {}
        ys_h = {}

        def l1_tanh(k, i):
            t = i
            xc, xs = x_codes[k // 2]
            j = 4 * (k % 2) + t
            if i == 0:
                tanh_t = act.tile([P, 4, CHUNK], F32)
                tanhs[k] = tanh_t
            acc = bank(ps_l1)
            accs[(k, t)] = acc
            nc.tensor.matmul_mx(
                out=acc[:],
                lhsT=w1_c[:, j * P : (j + 1) * P].bitcast(FP8X4),
                lhsT_scale=w1_s[:, j * P : (j + 1) * P],
                rhs=xc[:].bitcast(FP8X4),
                rhs_scale=xs[:],
                start=True,
                stop=True,
            )
            nc.scalar.activation(
                out=tanhs[k][:, t, :], in_=acc[:], func=ACT.Tanh, bias=b1_f[:, j : j + 1], scale=1.0
            )

        def add_tanh(k, t):
            if t == 0:
                y_t = yh.tile([P, 4, CHUNK], F32)
                ys_h[k] = y_t
            nc.vector.scalar_tensor_tensor(
                out=ys_h[k][:, t, :], in0=tanhs[k][:, t, :], scalar=1.0 / 9.0, in1=accs[(k, t)][:],
                op0=ALU.mult, op1=ALU.add,
            )

        def affine(k, t):
            j = 4 * (k % 2) + t
            y = ys_h[k][:, t, :]
            if affine_engine(k, t) == "S":
                nc.scalar.activation(out=y, in_=y, func=ACT.Identity, bias=b1_18[:, j : j + 1], scale=1.8)
            else:
                (nc.gpsimd if affine_engine(k, t) == "G" else nc.vector).tensor_scalar(
                    out=y, in0=y, scalar1=1.8, scalar2=b1_18[:, j : j + 1], op0=ALU.mult, op1=ALU.add
                )

        def affine_engine(k, t):
            return ("GGGS" if k < 13 else "GGSS")[t]

        def h_max(k):
            hg = hgp.tile([P, 4 * CHUNK], BF16, align_bytes=64)
            hgs[k] = hg
            nc.vector.tensor_tensor(
                out=hg[:].rearrange("p (c i t) -> p c t i", i=8, t=4),
                in0=ys_h[k][:].rearrange("p t (c i) -> p c t i", i=8),
                in1=tanhs[k][:].rearrange("p t (c i) -> p c t i", i=8),
                op=ALU.max,
            )

        def h_quant(k):
            hc = hcp.tile([P, CHUNK], U32, align_bytes=64)
            hs = hcp.tile([P, CHUNK], U8, align_bytes=64)
            nc.vector.quantize_mx(out=hc[:].bitcast(FP8X4), scales=hs[:], in_=hgs[k][:])
            h_codes[k] = (hc, hs)

        out_view = out.rearrange("(c p q) f -> c p q f", p=P, q=4)
        ys = {}

        def product_pass(acc2, c, fo, g):
            hc, hs = h_codes[2 * c + g]
            nc.tensor.matmul_mx(
                out=acc2[:],
                lhsT=w2_c[:, g, fo * P : (fo + 1) * P].bitcast(FP8X4),
                lhsT_scale=w2_s[:, g, fo * P : (fo + 1) * P],
                rhs=hc[:].bitcast(FP8X4),
                rhs_scale=hs[:],
                start=(g == 0),
                stop=(g == 1),
            )

        def add_bias(acc2, c, fo, on_vector):
            y_t = yp.tile([P, CHUNK], F32)
            ys[(c, fo)] = y_t
            if on_vector:
                nc.vector.tensor_scalar(
                    out=y_t[:], in0=acc2[:], scalar1=0.5, scalar2=b2_f[:, fo : fo + 1],
                    op0=ALU.mult, op1=ALU.add,
                )
            else:
                nc.scalar.activation(
                    out=y_t[:], in_=acc2[:], func=ACT.Identity, bias=b2_f[:, fo : fo + 1], scale=0.5
                )

        def back(c, fo, pool, on_vector):
            turn(c, fo, pool)
            leave(c, fo, on_vector)

        turned = {}

        def turn(c, fo, pool):
            tr = bank(pool)
            turned[(c, fo)] = tr
            for n in range(0, CHUNK, P):
                nc.tensor.transpose(tr[:, n : n + P], ys[(c, fo)][:, n : n + P], ident[:])

        def leave(c, fo, on_vector):
            tr = turned[(c, fo)]
            o_t = outp.tile([P, CHUNK], F32)
            if on_vector:
                nc.vector.tensor_scalar_max(out=o_t[:], in0=tr[:], scalar1=0.0)
            else:
                nc.scalar.activation(out=o_t[:], in_=tr[:], func=ACT.Relu)
            nc.sync.dma_start(
                out=out_view[c][:, :, fo * P : (fo + 1) * P],
                in_=o_t[:].rearrange("p (q f) -> p q f", f=P),
            )

        def product_n(n):
            acc2 = bank(ps)
            product_pass(acc2, n // N_OUT_TILES, n % N_OUT_TILES, 0)
            product_pass(acc2, n // N_OUT_TILES, n % N_OUT_TILES, 1)
            add_bias(acc2, n // N_OUT_TILES, n % N_OUT_TILES, False)

        def back_n(n):
            turn(n // N_OUT_TILES, n % N_OUT_TILES, ps)
            if n not in (16, 18):
                leave(n // N_OUT_TILES, n % N_OUT_TILES, False)

        regroup(nc.vector.tensor_copy, w1_g[:, 0:256, :], w1_raw[0][:])
        x_half(0, 0, ps)
        x_half(0, 1, ps)
        quant_w1(0, 256)
        b_rows_f = const.tile([P, P], F32)
        nc.vector.tensor_copy(out=b_rows_f[:], in_=b_rows[:])
        b_cols = bank(ps)
        nc.tensor.transpose(b_cols[:, 0:P], b_rows_f[:], ident[:])
        x_quant(0, 0)
        regroup(nc.vector.tensor_copy, w1_g[:, 256:512, :], w1_raw[1][:])
        x_quant(0, 1)
        nc.vector.tensor_copy(out=b1_f[:], in_=b_cols[:, 0:8])
        nc.vector.tensor_scalar_mul(out=b1_18[:], in0=b_cols[:, 0:8], scalar1=1.8)
        nc.vector.tensor_copy(out=b2_f[:], in_=b_cols[:, 8:12])
        quant_w1(256, 512)
        regroup(nc.scalar.copy, w1_g[:, 512:768, :], w1_raw[2][:, :, 0:256])
        regroup(nc.vector.tensor_copy, w1_g[:, 768:1024, :], w1_raw[2][:, :, 256:512])
        l1_tanh(0, 0)
        l1_tanh(0, 1)
        quant_w1(512, 1024)
        l1_tanh(0, 2)
        l1_tanh(0, 3)
        x_half(1, 0, ps)
        x_half(1, 1, ps)

        def products_until(s):
            return 4 * (N_CHUNKS - 1) if s == N_GROUPS - 1 else max(0, 2 * (s - 2))

        for s in range(N_GROUPS):
            for t in range(4):
                add_tanh(s, t)
                if s + 1 < N_GROUPS:
                    l1_tanh(s + 1, t)
                if affine_engine(s, t) == "G":
                    affine(s, t)
            for t in range(4):
                if s >= 1 and affine_engine(s - 1, t) == "V":
                    affine(s - 1, t)
                if affine_engine(s, t) == "S":
                    affine(s, t)
            if s >= 1:
                h_max(s - 1)
            for half_chunk in range(2 if s == 0 else s + 3, min(s + 4, 2 * N_CHUNKS)):
                x_quant(half_chunk // 2, half_chunk % 2)
            if s == 3:
                quant_w2(0)
                quant_w2(1)
            if s in (13, 14):
                n = products_until(s - 3)
                leave(n // N_OUT_TILES, n % N_OUT_TILES, True)
            if s >= 1:
                h_quant(s - 1)
            for n in range(products_until(s - 1), products_until(s)):
                product_n(n)
            backs = list(range(products_until(s - 2), products_until(s - 1)))
            for n in backs[:1]:
                back_n(n)
            if s in (1, 2):
                regroup(nc.scalar.copy, w2_g[:, s - 1, :, :], w2_raw[:, 4 * s - 4 : 4 * s, :])
            for n in backs[1:]:
                back_n(n)
            for half_chunk in range(4 if s == 0 else s + 6, min(s + 7, 2 * N_CHUNKS)):
                x_half(half_chunk // 2, half_chunk % 2, ps)

        last = N_CHUNKS - 1
        for t in range(4):
            if affine_engine(N_GROUPS - 1, t) == "V":
                affine(N_GROUPS - 1, t)
        h_max(N_GROUPS - 1)
        h_quant(N_GROUPS - 1)
        backs = list(range(products_until(N_GROUPS - 2), products_until(N_GROUPS - 1)))
        for n in backs[:1]:
            back_n(n)
        last_acc = []
        for fo in range(N_OUT_TILES):
            last_acc.append(bank(ps_l1))
            product_pass(last_acc[fo], last, fo, 0)
        for n in backs[1:4]:
            back_n(n)
        for fo in range(N_OUT_TILES):
            product_pass(last_acc[fo], last, fo, 1)
            add_bias(last_acc[fo], last, fo, fo % 2 == 0)
        for n in backs[4:]:
            back_n(n)
        for fo in range(N_OUT_TILES):
            back(last, fo, ps, fo % 2 == 0)
